import numpy as np
import ml_dtypes


def mxq(x, axis, fmt="e4m3"):
    dtype, down = {"e4m3": (ml_dtypes.float8_e4m3fn, 7), "e5m2": (ml_dtypes.float8_e5m2, 14)}[fmt]
    v = np.moveaxis(np.asarray(x, np.float32).astype(ml_dtypes.bfloat16).astype(np.float64), axis, -1)
    blocks = v.reshape(v.shape[:-1] + (-1, 32))
    amax = np.abs(blocks).max(-1, keepdims=True)
    byte = np.maximum(np.where(amax > 0, np.frexp(amax)[1] - 1 + 127, 0) - down, 1)
    scale = np.exp2(byte - 127.0)
    codes = (blocks / scale).astype(np.float32).astype(dtype).astype(np.float64)
    return np.moveaxis((codes * scale).reshape(v.shape), -1, axis)


WIDE = False


def mx_kscale(k):
    if not WIDE:
        return np.ones(k)
    levels = np.array([10, -10, 5, -5, 0])
    a = np.random.permutation(np.resize(levels, k // 512 * 4)).reshape(k // 512, 4)
    idx = np.arange(k)
    return np.exp2(a[idx // 512, idx % 128 // 32])


BF16 = ml_dtypes.bfloat16


def bf(x):
    return np.asarray(x, np.float32).astype(BF16)


def f64(x):
    return np.asarray(x).astype(np.float64)


N, D, H, HD = 1024, 1024, 16, 72
P = H * HD
HALF = HD // 2
EPS = 1e-6


def rms_norm(y):
    ms = np.mean(y * y, axis=-1, keepdims=True) + EPS
    return y * (1.0 / np.sqrt(ms))


def rotate_half(z):
    h = z.shape[-1] // 2
    return np.concatenate([-z[..., h:], z[..., :h]], axis=-1)


def rope_2d(y, cos, sin):
    def ap(z, c, s):
        return z * c[:, None, :] + rotate_half(z) * s[:, None, :]

    return np.concatenate([ap(y[..., :HALF], cos[:, :HALF], sin[:, :HALF]), ap(y[..., HALF:], cos[:, HALF:], sin[:, HALF:])], axis=-1)


def setup_inputs():
    s = mx_kscale(D)
    return {
        "hidden_states": bf(np.random.standard_normal((N, D)) * s),
        "cos": bf(np.random.uniform(-1.0, 1.0, (N, HD))),
        "sin": bf(np.random.uniform(-1.0, 1.0, (N, HD))),
        "Wq": bf(np.random.standard_normal((D, P)) / np.sqrt(D) / s[:, None]),
        "Wk": bf(np.random.standard_normal((D, P)) / np.sqrt(D) / s[:, None]),
        "Wv": bf(np.random.standard_normal((D, P)) / np.sqrt(D) / s[:, None]),
        "q_scale": bf(1.0 + 0.1 * np.random.standard_normal(HD)),
        "k_scale": bf(1.0 + 0.1 * np.random.standard_normal(HD)),
    }


def reference(hidden_states, cos, sin, Wq, Wk, Wv, q_scale, k_scale):
    x = mxq(f64(hidden_states), 1, "e4m3")
    c, s = f64(cos), f64(sin)
    yq = (x @ mxq(f64(Wq), 0, "e4m3")).reshape(N, H, HD)
    yk = (x @ mxq(f64(Wk), 0, "e4m3")).reshape(N, H, HD)
    yv = (x @ mxq(f64(Wv), 0, "e4m3")).reshape(N, H, HD)
    q = rms_norm(yq) * f64(q_scale)
    k = rms_norm(yk) * f64(k_scale)
    v = rms_norm(yv)
    return rope_2d(q, c, s), rope_2d(k, c, s), v

@@ -1,0 +1,250 @@
+from contextlib import ExitStack
+
+import concourse.mybir as mybir
+from concourse.masks import make_identity
+
+F32 = mybir.dt.float32
+BF16 = mybir.dt.bfloat16
+U32 = mybir.dt.uint32
+U8 = mybir.dt.uint8
+FP8X4 = mybir.dt.float8_e4m3fn_x4
+MULT = mybir.AluOpType.mult
+ADD = mybir.AluOpType.add
+ACT = mybir.ActivationFunctionType
+
+P = 128
+TOKENS = 1024
+D_MODEL = 1024
+HEADS = 16
+HEAD_DIM = 72
+FEATURES = HEADS * HEAD_DIM
+ROT = HEAD_DIM // 4
+EPS = 1e-6
+
+TILES = TOKENS // P
+PACK = 4
+PASSES = D_MODEL // (P * PACK)
+BANK = 512
+
+WINDOWS = ((0, 7, 0, 512), (7, 7, 504, 512), (14, 2, 896, 256))
+SLOTS = (0, 512, 1024)
+SLOT_COLUMNS = 1280
+
+FLOPS = 2 * TOKENS * D_MODEL * 3 * FEATURES
+
+
+def tile_torchgemma4visionattention_pa_kernel(
+    tc, hidden_states, cos, sin, Wq, Wk, Wv, q_scale, k_scale, out_0, out_1, out_2
+):
+    nc = tc.nc
+    weights = {"q": Wq, "k": Wk, "v": Wv}
+    gains = {"q": q_scale, "k": k_scale}
+    outputs = {"q": out_0, "k": out_1, "v": out_2}
+
+    with ExitStack() as ctx:
+        keep = ctx.enter_context(tc.tile_pool(name="keep", bufs=1))
+        stage = ctx.enter_context(tc.tile_pool(name="stage", bufs=3))
+        work = ctx.enter_context(tc.tile_pool(name="work", bufs=3))
+        psum = ctx.enter_context(tc.psum_pool(name="psum", bufs=8))
+
+        x_sb = keep.tile([P, TILES, D_MODEL], BF16, name="x_sb")
+        x_rows = hidden_states.rearrange("(p t) k -> p t k", t=TILES)
+        half = TILES // 2
+
+        w_raw = {}
+        for name in ("q", "k", "v"):
+            w_raw[name] = keep.tile([P, PASSES, PACK, FEATURES], BF16, name="w_raw_" + name)
+
+        def load_weight(name, g):
+            rows = weights[name][g * P * PACK : (g + 1) * P * PACK, :]
+            nc.sync.dma_start(
+                out=w_raw[name][:, g, :, :].rearrange("p (u e) c -> p u e c", e=2),
+                in_=rows.rearrange("(u p e) c -> p u e c", u=2, e=2),
+            )
+
+        nc.sync.dma_start(out=x_sb[:, 0:half, :], in_=x_rows[:, 0:half, :])
+        load_weight("q", 0)
+        load_weight("q", 1)
+        nc.sync.dma_start(out=x_sb[:, half:TILES, :], in_=x_rows[:, half:TILES, :])
+        for name in ("k", "v"):
+            for g in range(PASSES):
+                load_weight(name, g)
+
+        cos_sb = keep.tile([P, TILES, HEAD_DIM], BF16, name="cos_sb")
+        sin_sb = keep.tile([P, TILES, HEAD_DIM], BF16, name="sin_sb")
+        nc.scalar.dma_start(out=cos_sb[:], in_=cos.rearrange("(p t) j -> p t j", t=TILES))
+        nc.scalar.dma_start(out=sin_sb[:], in_=sin.rearrange("(p t) j -> p t j", t=TILES))
+        gain_sb = {}
+        for name in ("q", "k"):
+            gain_sb[name] = keep.tile([P, HEAD_DIM], BF16, name="gain_" + name)
+            nc.scalar.dma_start(out=gain_sb[name][:], in_=gains[name].partition_broadcast(P))
+
+        ident = keep.tile([P, P], F32, name="ident")
+        make_identity(nc, ident[:])
+        eps_sb = keep.tile([P, 1], F32, name="eps_sb")
+        nc.vector.memset(eps_sb[:], EPS)
+        warm = keep.tile([P, 1], F32, name="warm")
+        nc.scalar.activation(out=warm[:], in_=eps_sb[:], func=ACT.Sqrt)
+
+        stay = {}
+        cross = {}
+        for name in ("q", "k"):
+            signed = keep.tile([P, 2, 2, ROT], F32, name="signed_" + name)
+            gain4 = gain_sb[name][:].rearrange("p (a b i) -> p a b i", a=2, b=2)
+            nc.gpsimd.tensor_scalar(
+                out=signed[:, :, 0, :], in0=gain4[:, :, 0, :], scalar1=1.0, scalar2=0.0, op0=MULT, op1=ADD
+            )
+            nc.gpsimd.tensor_scalar(
+                out=signed[:, :, 1, :], in0=gain4[:, :, 1, :], scalar1=-1.0, scalar2=0.0, op0=MULT, op1=ADD
+            )
+            stay[name] = keep.tile([P, TILES, HEAD_DIM], F32, name="stay_" + name)
+            nc.gpsimd.tensor_tensor(
+                out=stay[name][:],
+                in0=cos_sb[:],
+                in1=gain_sb[name][:].unsqueeze(1).to_broadcast([P, TILES, HEAD_DIM]),
+                op=MULT,
+            )
+            cross[name] = keep.tile([P, TILES, HEAD_DIM], F32, name="cross_" + name)
+            cross5 = cross[name][:].rearrange("p t (a b i) -> p t a b i", a=2, b=2)
+            sin5 = sin_sb[:].rearrange("p t (a b i) -> p t a b i", a=2, b=2)
+            for b in range(2):
+                nc.gpsimd.tensor_tensor(
+                    out=cross5[:, :, :, b, :],
+                    in0=sin5[:, :, :, 1 - b, :],
+                    in1=signed[:, :, b, :].unsqueeze(1).to_broadcast([P, TILES, 2, ROT]),
+                    op=MULT,
+                )
+
+        x_codes = keep.tile([P, TILES, PASSES * P], U32, name="x_codes", align_bytes=64)
+        x_scales = keep.tile([P, TILES, PASSES * P], U8, name="x_scales", align_bytes=64)
+
+        def prepare_tokens(t):
+            x_words = x_sb[:, t, :].bitcast(F32)
+            turned = psum.tile([P, BANK], F32, name="turned", tag="bank")
+            for w in range(PASSES * 2):
+                nc.tensor.transpose(turned[:, w * P : (w + 1) * P], x_words[:, w * P : (w + 1) * P], ident[:])
+            x_grouped = stage.tile([P, PASSES, P, PACK], BF16, name="x_grouped", align_bytes=64)
+            nc.scalar.copy(
+                out=x_grouped[:].bitcast(F32),
+                in_=turned[:].rearrange("p (g u r) -> p g r u", g=PASSES, u=2),
+            )
+            nc.vector.quantize_mx(
+                out=x_codes[:, t, :].bitcast(FP8X4),
+                scales=x_scales[:, t, :],
+                in_=x_grouped[:].rearrange("p g r f -> p (g r f)"),
+            )
+
+        w_codes = {}
+        w_scales = {}
+        for name in ("q", "k", "v"):
+            w_codes[name] = keep.tile([P, PASSES, SLOT_COLUMNS], U32, name="w_codes_" + name, align_bytes=64)
+            w_scales[name] = keep.tile([P, PASSES, SLOT_COLUMNS], U8, name="w_scales_" + name, align_bytes=64)
+
+        def prepare_weights(name, g, i):
+            first_head, heads, col, width = WINDOWS[i]
+            slot = SLOTS[i]
+            w_grouped = stage.tile([P, BANK, PACK], BF16, name="w_grouped", align_bytes=64)
+            dst = w_grouped[:, 0:width, :].rearrange("p (c n) f -> p c f n", n=4)
+            src = w_raw[name][:, g, :, col : col + width].rearrange("p f (c n) -> p c f n", n=4)
+            if g == 0:
+                nc.vector.tensor_copy(out=dst, in_=src)
+            else:
+                nc.scalar.copy(out=dst, in_=src)
+            nc.vector.quantize_mx(
+                out=w_codes[name][:, g, slot : slot + width].bitcast(FP8X4),
+                scales=w_scales[name][:, g, slot : slot + width],
+                in_=w_grouped[:, 0:width, :].rearrange("p c f -> p (c f)"),
+            )
+
+        def project(name, t):
+            banks = []
+            for i in range(len(WINDOWS)):
+                banks.append(psum.tile([P, BANK], F32, name="y", tag="bank"))
+            for g in range(PASSES):
+                for i in range(len(WINDOWS)):
+                    width = WINDOWS[i][3]
+                    slot = SLOTS[i]
+                    nc.tensor.matmul_mx(
+                        out=banks[i][:, 0:width],
+                        lhsT=x_codes[:, t, g * P : (g + 1) * P].bitcast(FP8X4),
+                        lhsT_scale=x_scales[:, t, g * P : (g + 1) * P],
+                        rhs=w_codes[name][:, g, slot : slot + width].bitcast(FP8X4),
+                        rhs_scale=w_scales[name][:, g, slot : slot + width],
+                        start=(g == 0),
+                        stop=(g == PASSES - 1),
+                    )
+
+            def heads_of(i, first, count):
+                first_head, heads, col, width = WINDOWS[i]
+                begin = first * HEAD_DIM - col
+                return banks[i][:, begin : begin + count * HEAD_DIM]
+
+            squares = work.tile([P, FEATURES], BF16, name="squares")
+            sumsq = work.tile([P, HEADS], F32, name="sumsq")
+            for i in range(len(WINDOWS)):
+                first_head, heads, col, width = WINDOWS[i]
+                for h in range(first_head, first_head + heads):
+                    nc.scalar.activation(
+                        out=squares[:, h * HEAD_DIM : (h + 1) * HEAD_DIM],
+                        in_=heads_of(i, h, 1),
+                        func=ACT.Square,
+                        accum_out=sumsq[:, h : h + 1],
+                    )
+            rms = work.tile([P, HEADS], F32, name="rms")
+            nc.scalar.activation(out=rms[:], in_=sumsq[:], func=ACT.Sqrt, scale=1.0 / HEAD_DIM, bias=eps_sb[:])
+            rstd = work.tile([P, HEADS], F32, name="rstd")
+            nc.vector.reciprocal(out=rstd[:], in_=rms[:])
+
+            result = work.tile([P, FEATURES], F32, name="result")
+            if name == "v":
+                for i in range(len(WINDOWS)):
+                    first_head, heads, col, width = WINDOWS[i]
+                    nc.vector.tensor_tensor(
+                        out=result[:, first_head * HEAD_DIM : (first_head + heads) * HEAD_DIM].rearrange(
+                            "p (h j) -> p h j", j=HEAD_DIM
+                        ),
+                        in0=heads_of(i, first_head, heads).rearrange("p (h j) -> p h j", j=HEAD_DIM),
+                        in1=rstd[:, first_head : first_head + heads].unsqueeze(2).to_broadcast([P, heads, HEAD_DIM]),
+                        op=MULT,
+                    )
+            else:
+                own = work.tile([P, FEATURES], F32, name="own")
+                partner = work.tile([P, FEATURES], F32, name="partner")
+                for i in range(len(WINDOWS)):
+                    first_head, heads, col, width = WINDOWS[i]
+                    for h in range(first_head, first_head + heads):
+                        for table, product in ((stay, own), (cross, partner)):
+                            nc.vector.scalar_tensor_tensor(
+                                out=product[:, h * HEAD_DIM : (h + 1) * HEAD_DIM],
+                                in0=heads_of(i, h, 1),
+                                scalar=rstd[:, h : h + 1],
+                                in1=table[name][:, t, :],
+                                op0=MULT,
+                                op1=MULT,
+                            )
+                result4 = result[:].rearrange("p (m b i) -> p m b i", b=2, i=ROT)
+                own4 = own[:].rearrange("p (m b i) -> p m b i", b=2, i=ROT)
+                partner4 = partner[:].rearrange("p (m b i) -> p m b i", b=2, i=ROT)
+                for b in range(2):
+                    nc.gpsimd.tensor_tensor(
+                        out=result4[:, :, b, :], in0=own4[:, :, b, :], in1=partner4[:, :, 1 - b, :], op=ADD
+                    )
+            nc.sync.dma_start(
+                out=outputs[name].rearrange("(p t) h j -> p t (h j)", t=TILES)[:, t, :], in_=result[:]
+            )
+
+        for t in range(TILES):
+            prepare_tokens(t)
+        for i in range(len(WINDOWS)):
+            for g in range(PASSES):
+                prepare_weights("q", g, i)
+        for t in range(TILES):
+            project("q", t)
+            if t == 0:
+                for name in ("k", "v"):
+                    for i in range(len(WINDOWS)):
+                        for g in range(PASSES):
+                            prepare_weights(name, g, i)
+        for t in range(TILES):
+            project("k", t)
+            project("v", t)

@@ -5,6 +5,7 @@ from concourse.masks import make_identity
 
 F32 = mybir.dt.float32
 BF16 = mybir.dt.bfloat16
+I32 = mybir.dt.int32
 U32 = mybir.dt.uint32
 U8 = mybir.dt.uint8
 FP8X4 = mybir.dt.float8_e4m3fn_x4
@@ -23,12 +24,15 @@ EPS = 1e-6
 
 TILES = TOKENS // P
 PACK = 4
-PASSES = D_MODEL // (P * PACK)
+K_PASS = P * PACK
+PASSES = D_MODEL // K_PASS
 BANK = 512
 
-WINDOWS = ((0, 7, 0, 512), (7, 7, 504, 512), (14, 2, 896, 256))
+WINDOWS = ((0, 7, 512), (7, 7, 512), (14, 2, 256))
 SLOTS = (0, 512, 1024)
 SLOT_COLUMNS = 1280
+PIECES = ((0, 512), (512, 512), (1024, 128))
+AHEAD = 2
 
 FLOPS = 2 * TOKENS * D_MODEL * 3 * FEATURES
 
@@ -42,6 +46,7 @@ def tile_torchgemma4visionattention_pa_kernel(
     outputs = {"q": out_0, "k": out_1, "v": out_2}
 
     with ExitStack() as ctx:
+        ctx.enter_context(tc.manual_schedule())
         keep = ctx.enter_context(tc.tile_pool(name="keep", bufs=1))
         stage = ctx.enter_context(tc.tile_pool(name="stage", bufs=3))
         work = ctx.enter_context(tc.tile_pool(name="work", bufs=3))
@@ -49,26 +54,17 @@ def tile_torchgemma4visionattention_pa_kernel(
 
         x_sb = keep.tile([P, TILES, D_MODEL], BF16, name="x_sb")
         x_rows = hidden_states.rearrange("(p t) k -> p t k", t=TILES)
-        half = TILES // 2
 
         w_raw = {}
         for name in ("q", "k", "v"):
             w_raw[name] = keep.tile([P, PASSES, PACK, FEATURES], BF16, name="w_raw_" + name)
 
-        def load_weight(name, g):
-            rows = weights[name][g * P * PACK : (g + 1) * P * PACK, :]
+        def load_weight(name, g, first, count):
+            rows = weights[name][g * K_PASS : (g + 1) * K_PASS, first : first + count]
             nc.sync.dma_start(
-                out=w_raw[name][:, g, :, :].rearrange("p (u e) c -> p u e c", e=2),
-                in_=rows.rearrange("(u p e) c -> p u e c", u=2, e=2),
+                out=w_raw[name][:, g, :, first : first + count],
+                in_=rows.rearrange("(p f) c -> p f c", f=PACK),
             )
-
-        nc.sync.dma_start(out=x_sb[:, 0:half, :], in_=x_rows[:, 0:half, :])
-        load_weight("q", 0)
-        load_weight("q", 1)
-        nc.sync.dma_start(out=x_sb[:, half:TILES, :], in_=x_rows[:, half:TILES, :])
-        for name in ("k", "v"):
-            for g in range(PASSES):
-                load_weight(name, g)
 
         cos_sb = keep.tile([P, TILES, HEAD_DIM], BF16, name="cos_sb")
         sin_sb = keep.tile([P, TILES, HEAD_DIM], BF16, name="sin_sb")
@@ -79,33 +75,45 @@ def tile_torchgemma4visionattention_pa_kernel(
             gain_sb[name] = keep.tile([P, HEAD_DIM], BF16, name="gain_" + name)
             nc.scalar.dma_start(out=gain_sb[name][:], in_=gains[name].partition_broadcast(P))
 
+        for first, count in PIECES:
+            for g in (1, 0):
+                load_weight("q", g, first, count)
+        nc.sync.dma_start(out=x_sb[:, 0:AHEAD, :], in_=x_rows[:, 0:AHEAD, :])
+        for name in ("k", "v"):
+            for g in (1, 0):
+                load_weight(name, g, 0, FEATURES)
+        nc.sync.dma_start(out=x_sb[:, AHEAD:TILES, :], in_=x_rows[:, AHEAD:TILES, :])
+
         ident = keep.tile([P, P], F32, name="ident")
         make_identity(nc, ident[:])
         eps_sb = keep.tile([P, 1], F32, name="eps_sb")
         nc.vector.memset(eps_sb[:], EPS)
         warm = keep.tile([P, 1], F32, name="warm")
-        nc.scalar.activation(out=warm[:], in_=eps_sb[:], func=ACT.Sqrt)
+        nc.scalar.activation(out=warm[:], in_=eps_sb[:], func=ACT.Abs_reciprocal_sqrt)
 
-        stay = {}
-        cross = {}
+        w_stage = {}
+        for i in range(len(WINDOWS)):
+            first_head, heads, width = WINDOWS[i]
+            for g in range(PASSES):
+                w_stage[(i, g)] = keep.tile([P, width, PACK], BF16, name="w_stage_%d_%d" % (i, g), align_bytes=64)
+                nc.vector.memset(w_stage[(i, g)][:, heads * HEAD_DIM : width, :].bitcast(I32), 0)
+
+        rope = {}
         for name in ("q", "k"):
             signed = keep.tile([P, 2, 2, ROT], F32, name="signed_" + name)
             gain4 = gain_sb[name][:].rearrange("p (a b i) -> p a b i", a=2, b=2)
-            nc.gpsimd.tensor_scalar(
-                out=signed[:, :, 0, :], in0=gain4[:, :, 0, :], scalar1=1.0, scalar2=0.0, op0=MULT, op1=ADD
-            )
-            nc.gpsimd.tensor_scalar(
-                out=signed[:, :, 1, :], in0=gain4[:, :, 1, :], scalar1=-1.0, scalar2=0.0, op0=MULT, op1=ADD
-            )
-            stay[name] = keep.tile([P, TILES, HEAD_DIM], F32, name="stay_" + name)
+            for b, sign in ((0, 1.0), (1, -1.0)):
+                nc.gpsimd.tensor_scalar(
+                    out=signed[:, :, b, :], in0=gain4[:, :, b, :], scalar1=sign, scalar2=0.0, op0=MULT, op1=ADD
+                )
+            rope[name] = keep.tile([P, TILES, 2, HEAD_DIM], F32, name="rope_" + name)
             nc.gpsimd.tensor_tensor(
-                out=stay[name][:],
+                out=rope[name][:, :, 0, :],
                 in0=cos_sb[:],
                 in1=gain_sb[name][:].unsqueeze(1).to_broadcast([P, TILES, HEAD_DIM]),
                 op=MULT,
             )
-            cross[name] = keep.tile([P, TILES, HEAD_DIM], F32, name="cross_" + name)
-            cross5 = cross[name][:].rearrange("p t (a b i) -> p t a b i", a=2, b=2)
+            cross5 = rope[name][:, :, 1, :].rearrange("p t (a b i) -> p t a b i", a=2, b=2)
             sin5 = sin_sb[:].rearrange("p t (a b i) -> p t a b i", a=2, b=2)
             for b in range(2):
                 nc.gpsimd.tensor_tensor(
@@ -119,15 +127,13 @@ def tile_torchgemma4visionattention_pa_kernel(
         x_scales = keep.tile([P, TILES, PASSES * P], U8, name="x_scales", align_bytes=64)
 
         def prepare_tokens(t):
-            x_words = x_sb[:, t, :].bitcast(F32)
-            turned = psum.tile([P, BANK], F32, name="turned", tag="bank")
-            for w in range(PASSES * 2):
-                nc.tensor.transpose(turned[:, w * P : (w + 1) * P], x_words[:, w * P : (w + 1) * P], ident[:])
+            x_words = x_sb[:, t, :].bitcast(F32).rearrange("r (g p u) -> r g u p", g=PASSES, u=2)
+            turned = psum.tile([P, PASSES, 2, P], F32, name="turned", tag="bank")
+            for g in range(PASSES):
+                for u in range(2):
+                    nc.tensor.transpose(turned[:, g, u, :], x_words[:, g, u, :], ident[:])
             x_grouped = stage.tile([P, PASSES, P, PACK], BF16, name="x_grouped", align_bytes=64)
-            nc.scalar.copy(
-                out=x_grouped[:].bitcast(F32),
-                in_=turned[:].rearrange("p (g u r) -> p g r u", g=PASSES, u=2),
-            )
+            nc.scalar.copy(out=x_grouped[:].bitcast(F32), in_=turned[:].rearrange("p g u r -> p g r u"))
             nc.vector.quantize_mx(
                 out=x_codes[:, t, :].bitcast(FP8X4),
                 scales=x_scales[:, t, :],
@@ -140,30 +146,44 @@ def tile_torchgemma4visionattention_pa_kernel(
             w_codes[name] = keep.tile([P, PASSES, SLOT_COLUMNS], U32, name="w_codes_" + name, align_bytes=64)
             w_scales[name] = keep.tile([P, PASSES, SLOT_COLUMNS], U8, name="w_scales_" + name, align_bytes=64)
 
-        def prepare_weights(name, g, i):
-            first_head, heads, col, width = WINDOWS[i]
+        def regroup(name, i):
+            first_head, heads, width = WINDOWS[i]
+            first = first_head * HEAD_DIM
+            count = heads * HEAD_DIM
+
+            def side_by_side(g):
+                return w_stage[(i, g)][:, 0:count, :].rearrange("p (c n) f -> p c f n", n=4)
+
+            def row_by_row(g):
+                return w_raw[name][:, g, :, first : first + count].rearrange("p f (c n) -> p c f n", n=4)
+
+            nc.scalar.copy(out=side_by_side(1), in_=row_by_row(1))
+            nc.vector.tensor_copy(out=side_by_side(0), in_=row_by_row(0))
+
+        def quantise(name, i):
+            width = WINDOWS[i][2]
             slot = SLOTS[i]
-            w_grouped = stage.tile([P, BANK, PACK], BF16, name="w_grouped", align_bytes=64)
-            dst = w_grouped[:, 0:width, :].rearrange("p (c n) f -> p c f n", n=4)
-            src = w_raw[name][:, g, :, col : col + width].rearrange("p f (c n) -> p c f n", n=4)
-            if g == 0:
-                nc.vector.tensor_copy(out=dst, in_=src)
-            else:
-                nc.scalar.copy(out=dst, in_=src)
-            nc.vector.quantize_mx(
-                out=w_codes[name][:, g, slot : slot + width].bitcast(FP8X4),
-                scales=w_scales[name][:, g, slot : slot + width],
-                in_=w_grouped[:, 0:width, :].rearrange("p c f -> p (c f)"),
-            )
+            for g in (1, 0):
+                nc.vector.quantize_mx(
+                    out=w_codes[name][:, g, slot : slot + width].bitcast(FP8X4),
+                    scales=w_scales[name][:, g, slot : slot + width],
+                    in_=w_stage[(i, g)][:].rearrange("p c f -> p (c f)"),
+                )
+
+        def prepare_weights(name):
+            for i in range(len(WINDOWS) + 1):
+                if i < len(WINDOWS):
+                    regroup(name, i)
+                if i > 0:
+                    quantise(name, i - 1)
 
         def project(name, t):
             banks = []
             for i in range(len(WINDOWS)):
+                width = WINDOWS[i][2]
+                slot = SLOTS[i]
                 banks.append(psum.tile([P, BANK], F32, name="y", tag="bank"))
-            for g in range(PASSES):
-                for i in range(len(WINDOWS)):
-                    width = WINDOWS[i][3]
-                    slot = SLOTS[i]
+                for g in range(PASSES):
                     nc.tensor.matmul_mx(
                         out=banks[i][:, 0:width],
                         lhsT=x_codes[:, t, g * P : (g + 1) * P].bitcast(FP8X4),
@@ -174,77 +194,63 @@ def tile_torchgemma4visionattention_pa_kernel(
                         stop=(g == PASSES - 1),
                     )
 
-            def heads_of(i, first, count):
-                first_head, heads, col, width = WINDOWS[i]
-                begin = first * HEAD_DIM - col
-                return banks[i][:, begin : begin + count * HEAD_DIM]
-
-            squares = work.tile([P, FEATURES], BF16, name="squares")
+            squares = work.tile([P, HEADS, HEAD_DIM], BF16, name="squares", bufs=2)
             sumsq = work.tile([P, HEADS], F32, name="sumsq")
             for i in range(len(WINDOWS)):
-                first_head, heads, col, width = WINDOWS[i]
-                for h in range(first_head, first_head + heads):
+                first_head, heads, width = WINDOWS[i]
+                for h in range(heads):
                     nc.scalar.activation(
-                        out=squares[:, h * HEAD_DIM : (h + 1) * HEAD_DIM],
-                        in_=heads_of(i, h, 1),
+                        out=squares[:, first_head + h, :],
+                        in_=banks[i][:, h * HEAD_DIM : (h + 1) * HEAD_DIM],
                         func=ACT.Square,
-                        accum_out=sumsq[:, h : h + 1],
+                        accum_out=sumsq[:, first_head + h : first_head + h + 1],
                     )
-            rms = work.tile([P, HEADS], F32, name="rms")
-            nc.scalar.activation(out=rms[:], in_=sumsq[:], func=ACT.Sqrt, scale=1.0 / HEAD_DIM, bias=eps_sb[:])
             rstd = work.tile([P, HEADS], F32, name="rstd")
-            nc.vector.reciprocal(out=rstd[:], in_=rms[:])
+            nc.scalar.activation(
+                out=rstd[:], in_=sumsq[:], func=ACT.Abs_reciprocal_sqrt, scale=1.0 / HEAD_DIM, bias=eps_sb[:]
+            )
 
-            result = work.tile([P, FEATURES], F32, name="result")
+            result = work.tile([P, HEADS, HEAD_DIM], F32, name="result", bufs=5)
             if name == "v":
                 for i in range(len(WINDOWS)):
-                    first_head, heads, col, width = WINDOWS[i]
+                    first_head, heads, width = WINDOWS[i]
                     nc.vector.tensor_tensor(
-                        out=result[:, first_head * HEAD_DIM : (first_head + heads) * HEAD_DIM].rearrange(
-                            "p (h j) -> p h j", j=HEAD_DIM
-                        ),
-                        in0=heads_of(i, first_head, heads).rearrange("p (h j) -> p h j", j=HEAD_DIM),
+                        out=result[:, first_head : first_head + heads, :],
+                        in0=banks[i][:, 0 : heads * HEAD_DIM].rearrange("p (h j) -> p h j", j=HEAD_DIM),
                         in1=rstd[:, first_head : first_head + heads].unsqueeze(2).to_broadcast([P, heads, HEAD_DIM]),
                         op=MULT,
                     )
             else:
-                own = work.tile([P, FEATURES], F32, name="own")
-                partner = work.tile([P, FEATURES], F32, name="partner")
+                products = work.tile([P, HEADS, 2, HEAD_DIM], F32, name="products", bufs=2)
                 for i in range(len(WINDOWS)):
-                    first_head, heads, col, width = WINDOWS[i]
-                    for h in range(first_head, first_head + heads):
-                        for table, product in ((stay, own), (cross, partner)):
-                            nc.vector.scalar_tensor_tensor(
-                                out=product[:, h * HEAD_DIM : (h + 1) * HEAD_DIM],
-                                in0=heads_of(i, h, 1),
-                                scalar=rstd[:, h : h + 1],
-                                in1=table[name][:, t, :],
-                                op0=MULT,
-                                op1=MULT,
-                            )
-                result4 = result[:].rearrange("p (m b i) -> p m b i", b=2, i=ROT)
-                own4 = own[:].rearrange("p (m b i) -> p m b i", b=2, i=ROT)
-                partner4 = partner[:].rearrange("p (m b i) -> p m b i", b=2, i=ROT)
+                    first_head, heads, width = WINDOWS[i]
+                    for h in range(heads):
+                        nc.vector.scalar_tensor_tensor(
+                            out=products[:, first_head + h, :, :],
+                            in0=banks[i][:, h * HEAD_DIM : (h + 1) * HEAD_DIM].unsqueeze(1).to_broadcast([P, 2, HEAD_DIM]),
+                            scalar=rstd[:, first_head + h : first_head + h + 1],
+                            in1=rope[name][:, t, :, :],
+                            op0=MULT,
+                            op1=MULT,
+                        )
+                result5 = result[:].rearrange("p h (a b i) -> p h a b i", a=2, b=2)
+                products6 = products[:].rearrange("p h s (a b i) -> p h s a b i", a=2, b=2)
                 for b in range(2):
                     nc.gpsimd.tensor_tensor(
-                        out=result4[:, :, b, :], in0=own4[:, :, b, :], in1=partner4[:, :, 1 - b, :], op=ADD
+                        out=result5[:, :, :, b, :],
+                        in0=products6[:, :, 0, :, b, :],
+                        in1=products6[:, :, 1, :, 1 - b, :],
+                        op=ADD,
                     )
-            nc.sync.dma_start(
-                out=outputs[name].rearrange("(p t) h j -> p t (h j)", t=TILES)[:, t, :], in_=result[:]
-            )
+            nc.sync.dma_start(out=outputs[name].rearrange("(p t) h j -> p t h j", t=TILES)[:, t, :, :], in_=result[:])
 
-        for t in range(TILES):
+        prepare_weights("q")
+        for t in range(AHEAD):
             prepare_tokens(t)
-        for i in range(len(WINDOWS)):
-            for g in range(PASSES):
-                prepare_weights("q", g, i)
+        prepare_weights("k")
+        prepare_weights("v")
         for t in range(TILES):
-            project("q", t)
-            if t == 0:
-                for name in ("k", "v"):
-                    for i in range(len(WINDOWS)):
-                        for g in range(PASSES):
-                            prepare_weights(name, g, i)
-        for t in range(TILES):
-            project("k", t)
-            project("v", t)
+            for name in ("q", "k", "v"):
+                project(name, t)
+            if t + AHEAD < TILES:
+                prepare_tokens(t + AHEAD)

@@ -32,7 +32,7 @@ WINDOWS = ((0, 7, 512), (7, 7, 512), (14, 2, 256))
 SLOTS = (0, 512, 1024)
 SLOT_COLUMNS = 1280
 PIECES = ((0, 512), (512, 512), (1024, 128))
-AHEAD = 2
+PAIR = 2
 
 FLOPS = 2 * TOKENS * D_MODEL * 3 * FEATURES
 
@@ -78,11 +78,11 @@ def tile_torchgemma4visionattention_pa_kernel(
         for first, count in PIECES:
             for g in (1, 0):
                 load_weight("q", g, first, count)
-        nc.sync.dma_start(out=x_sb[:, 0:AHEAD, :], in_=x_rows[:, 0:AHEAD, :])
+        nc.sync.dma_start(out=x_sb[:, 0:PAIR, :], in_=x_rows[:, 0:PAIR, :])
         for name in ("k", "v"):
             for g in (1, 0):
                 load_weight(name, g, 0, FEATURES)
-        nc.sync.dma_start(out=x_sb[:, AHEAD:TILES, :], in_=x_rows[:, AHEAD:TILES, :])
+        nc.sync.dma_start(out=x_sb[:, PAIR:TILES, :], in_=x_rows[:, PAIR:TILES, :])
 
         ident = keep.tile([P, P], F32, name="ident")
         make_identity(nc, ident[:])
@@ -99,15 +99,16 @@ def tile_torchgemma4visionattention_pa_kernel(
                 nc.vector.memset(w_stage[(i, g)][:, heads * HEAD_DIM : width, :].bitcast(I32), 0)
 
         rope = {}
-        for name in ("q", "k"):
+
+        def build_rope_table(name):
             signed = keep.tile([P, 2, 2, ROT], F32, name="signed_" + name)
             gain4 = gain_sb[name][:].rearrange("p (a b i) -> p a b i", a=2, b=2)
             for b, sign in ((0, 1.0), (1, -1.0)):
-                nc.gpsimd.tensor_scalar(
+                nc.vector.tensor_scalar(
                     out=signed[:, :, b, :], in0=gain4[:, :, b, :], scalar1=sign, scalar2=0.0, op0=MULT, op1=ADD
                 )
             rope[name] = keep.tile([P, TILES, 2, HEAD_DIM], F32, name="rope_" + name)
-            nc.gpsimd.tensor_tensor(
+            nc.vector.tensor_tensor(
                 out=rope[name][:, :, 0, :],
                 in0=cos_sb[:],
                 in1=gain_sb[name][:].unsqueeze(1).to_broadcast([P, TILES, HEAD_DIM]),
@@ -116,7 +117,7 @@ def tile_torchgemma4visionattention_pa_kernel(
             cross5 = rope[name][:, :, 1, :].rearrange("p t (a b i) -> p t a b i", a=2, b=2)
             sin5 = sin_sb[:].rearrange("p t (a b i) -> p t a b i", a=2, b=2)
             for b in range(2):
-                nc.gpsimd.tensor_tensor(
+                nc.vector.tensor_tensor(
                     out=cross5[:, :, :, b, :],
                     in0=sin5[:, :, :, 1 - b, :],
                     in1=signed[:, :, b, :].unsqueeze(1).to_broadcast([P, TILES, 2, ROT]),
@@ -126,18 +127,19 @@ def tile_torchgemma4visionattention_pa_kernel(
         x_codes = keep.tile([P, TILES, PASSES * P], U32, name="x_codes", align_bytes=64)
         x_scales = keep.tile([P, TILES, PASSES * P], U8, name="x_scales", align_bytes=64)
 
-        def prepare_tokens(t):
-            x_words = x_sb[:, t, :].bitcast(F32).rearrange("r (g p u) -> r g u p", g=PASSES, u=2)
-            turned = psum.tile([P, PASSES, 2, P], F32, name="turned", tag="bank")
-            for g in range(PASSES):
-                for u in range(2):
-                    nc.tensor.transpose(turned[:, g, u, :], x_words[:, g, u, :], ident[:])
-            x_grouped = stage.tile([P, PASSES, P, PACK], BF16, name="x_grouped", align_bytes=64)
-            nc.scalar.copy(out=x_grouped[:].bitcast(F32), in_=turned[:].rearrange("p g u r -> p g r u"))
+        def prepare_tokens(first):
+            x_grouped = stage.tile([P, PAIR, PASSES, P, PACK], BF16, name="x_grouped", align_bytes=64)
+            for n in range(PAIR):
+                x_words = x_sb[:, first + n, :].bitcast(F32).rearrange("r (g p u) -> r g u p", g=PASSES, u=2)
+                turned = psum.tile([P, PASSES, 2, P], F32, name="turned", tag="bank")
+                for g in range(PASSES):
+                    for u in range(2):
+                        nc.tensor.transpose(turned[:, g, u, :], x_words[:, g, u, :], ident[:])
+                nc.scalar.copy(out=x_grouped[:, n].bitcast(F32), in_=turned[:].rearrange("p g u r -> p g r u"))
             nc.vector.quantize_mx(
-                out=x_codes[:, t, :].bitcast(FP8X4),
-                scales=x_scales[:, t, :],
-                in_=x_grouped[:].rearrange("p g r f -> p (g r f)"),
+                out=x_codes[:, first : first + PAIR, :].rearrange("p t c -> p (t c)").bitcast(FP8X4),
+                scales=x_scales[:, first : first + PAIR, :].rearrange("p t c -> p (t c)"),
+                in_=x_grouped[:].rearrange("p t g r f -> p (t g r f)"),
             )
 
         w_codes = {}
@@ -242,15 +244,22 @@ def tile_torchgemma4visionattention_pa_kernel(
                         in1=products6[:, :, 1, :, 1 - b, :],
                         op=ADD,
                     )
+            return result
+
+        def store(name, t, result):
             nc.sync.dma_start(out=outputs[name].rearrange("(p t) h j -> p t h j", t=TILES)[:, t, :, :], in_=result[:])
 
+        build_rope_table("q")
         prepare_weights("q")
-        for t in range(AHEAD):
-            prepare_tokens(t)
+        prepare_tokens(0)
+        build_rope_table("k")
         prepare_weights("k")
         prepare_weights("v")
         for t in range(TILES):
+            results = {}
             for name in ("q", "k", "v"):
-                project(name, t)
-            if t + AHEAD < TILES:
-                prepare_tokens(t + AHEAD)
+                results[name] = project(name, t)
+            for name in ("q", "v", "k"):
+                store(name, t, results[name])
+            if t % PAIR == 0 and t + PAIR < TILES:
+                prepare_tokens(t + PAIR)

@@ -28,9 +28,7 @@ K_PASS = P * PACK
 PASSES = D_MODEL // K_PASS
 BANK = 512
 
-WINDOWS = ((0, 7, 512), (7, 7, 512), (14, 2, 256))
-SLOTS = (0, 512, 1024)
-SLOT_COLUMNS = 1280
+WINDOWS = ((0, 512, 0, 7), (448, 512, 7, 6), (896, 256, 13, 3))
 PIECES = ((0, 512), (512, 512), (1024, 128))
 PAIR = 2
 
@@ -48,16 +46,21 @@ def tile_torchgemma4visionattention_pa_kernel(
     with ExitStack() as ctx:
         ctx.enter_context(tc.manual_schedule())
         keep = ctx.enter_context(tc.tile_pool(name="keep", bufs=1))
-        stage = ctx.enter_context(tc.tile_pool(name="stage", bufs=3))
+        raws = ctx.enter_context(tc.tile_pool(name="raws", bufs=3))
+        stage = ctx.enter_context(tc.tile_pool(name="stage", bufs=2))
         work = ctx.enter_context(tc.tile_pool(name="work", bufs=3))
         psum = ctx.enter_context(tc.psum_pool(name="psum", bufs=8))
 
         x_sb = keep.tile([P, TILES, D_MODEL], BF16, name="x_sb")
         x_rows = hidden_states.rearrange("(p t) k -> p t k", t=TILES)
 
+        def load_tokens(first, count):
+            nc.sync.dma_start(out=x_sb[:, first : first + count, :], in_=x_rows[:, first : first + count, :])
+
         w_raw = {}
-        for name in ("q", "k", "v"):
-            w_raw[name] = keep.tile([P, PASSES, PACK, FEATURES], BF16, name="w_raw_" + name)
+
+        def new_raw(name):
+            w_raw[name] = raws.tile([P, PASSES, PACK, FEATURES], BF16, name="w_raw")
 
         def load_weight(name, g, first, count):
             rows = weights[name][g * K_PASS : (g + 1) * K_PASS, first : first + count]
@@ -68,21 +71,23 @@ def tile_torchgemma4visionattention_pa_kernel(
 
         cos_sb = keep.tile([P, TILES, HEAD_DIM], BF16, name="cos_sb")
         sin_sb = keep.tile([P, TILES, HEAD_DIM], BF16, name="sin_sb")
-        nc.scalar.dma_start(out=cos_sb[:], in_=cos.rearrange("(p t) j -> p t j", t=TILES))
-        nc.scalar.dma_start(out=sin_sb[:], in_=sin.rearrange("(p t) j -> p t j", t=TILES))
+        nc.sync.dma_start(out=cos_sb[:], in_=cos.rearrange("(p t) j -> p t j", t=TILES))
+        nc.sync.dma_start(out=sin_sb[:], in_=sin.rearrange("(p t) j -> p t j", t=TILES))
         gain_sb = {}
         for name in ("q", "k"):
             gain_sb[name] = keep.tile([P, HEAD_DIM], BF16, name="gain_" + name)
-            nc.scalar.dma_start(out=gain_sb[name][:], in_=gains[name].partition_broadcast(P))
+            nc.sync.dma_start(out=gain_sb[name][:], in_=gains[name].partition_broadcast(P))
 
+        new_raw("q")
         for first, count in PIECES:
             for g in (1, 0):
                 load_weight("q", g, first, count)
-        nc.sync.dma_start(out=x_sb[:, 0:PAIR, :], in_=x_rows[:, 0:PAIR, :])
+        load_tokens(0, PAIR)
         for name in ("k", "v"):
+            new_raw(name)
             for g in (1, 0):
                 load_weight(name, g, 0, FEATURES)
-        nc.sync.dma_start(out=x_sb[:, PAIR:TILES, :], in_=x_rows[:, PAIR:TILES, :])
+        load_tokens(PAIR, TILES - PAIR)
 
         ident = keep.tile([P, P], F32, name="ident")
         make_identity(nc, ident[:])
@@ -90,13 +95,6 @@ def tile_torchgemma4visionattention_pa_kernel(
         nc.vector.memset(eps_sb[:], EPS)
         warm = keep.tile([P, 1], F32, name="warm")
         nc.scalar.activation(out=warm[:], in_=eps_sb[:], func=ACT.Abs_reciprocal_sqrt)
-
-        w_stage = {}
-        for i in range(len(WINDOWS)):
-            first_head, heads, width = WINDOWS[i]
-            for g in range(PASSES):
-                w_stage[(i, g)] = keep.tile([P, width, PACK], BF16, name="w_stage_%d_%d" % (i, g), align_bytes=64)
-                nc.vector.memset(w_stage[(i, g)][:, heads * HEAD_DIM : width, :].bitcast(I32), 0)
 
         rope = {}
 
@@ -127,7 +125,7 @@ def tile_torchgemma4visionattention_pa_kernel(
         x_codes = keep.tile([P, TILES, PASSES * P], U32, name="x_codes", align_bytes=64)
         x_scales = keep.tile([P, TILES, PASSES * P], U8, name="x_scales", align_bytes=64)
 
-        def prepare_tokens(first):
+        def turn_tokens(first):
             x_grouped = stage.tile([P, PAIR, PASSES, P, PACK], BF16, name="x_grouped", align_bytes=64)
             for n in range(PAIR):
                 x_words = x_sb[:, first + n, :].bitcast(F32).rearrange("r (g p u) -> r g u p", g=PASSES, u=2)
@@ -136,6 +134,9 @@ def tile_torchgemma4visionattention_pa_kernel(
                     for u in range(2):
                         nc.tensor.transpose(turned[:, g, u, :], x_words[:, g, u, :], ident[:])
                 nc.scalar.copy(out=x_grouped[:, n].bitcast(F32), in_=turned[:].rearrange("p g u r -> p g r u"))
+            return x_grouped
+
+        def quantise_tokens(first, x_grouped):
             nc.vector.quantize_mx(
                 out=x_codes[:, first : first + PAIR, :].rearrange("p t c -> p (t c)").bitcast(FP8X4),
                 scales=x_scales[:, first : first + PAIR, :].rearrange("p t c -> p (t c)"),
@@ -144,66 +145,58 @@ def tile_torchgemma4visionattention_pa_kernel(
 
         w_codes = {}
         w_scales = {}
-        for name in ("q", "k", "v"):
-            w_codes[name] = keep.tile([P, PASSES, SLOT_COLUMNS], U32, name="w_codes_" + name, align_bytes=64)
-            w_scales[name] = keep.tile([P, PASSES, SLOT_COLUMNS], U8, name="w_scales_" + name, align_bytes=64)
+        w_stage = {}
+        for name in ("q", "v", "k"):
+            w_codes[name] = keep.tile([P, PASSES, FEATURES], U32, name="w_codes_" + name, align_bytes=64)
+            w_scales[name] = keep.tile([P, PASSES, FEATURES], U8, name="w_scales_" + name, align_bytes=64)
 
-        def regroup(name, i):
-            first_head, heads, width = WINDOWS[i]
-            first = first_head * HEAD_DIM
-            count = heads * HEAD_DIM
+        def new_stage(name):
+            for g in range(PASSES):
+                w_stage[(name, g)] = stage.tile([P, FEATURES, PACK], BF16, name="w_stage_%d" % g, align_bytes=64)
 
-            def side_by_side(g):
-                return w_stage[(i, g)][:, 0:count, :].rearrange("p (c n) f -> p c f n", n=4)
+        def side_by_side(name, g, first, count):
+            return w_stage[(name, g)][:, first : first + count, :].rearrange("p (c n) f -> p c f n", n=4)
 
-            def row_by_row(g):
-                return w_raw[name][:, g, :, first : first + count].rearrange("p f (c n) -> p c f n", n=4)
+        def row_by_row(name, g, first, count):
+            return w_raw[name][:, g, :, first : first + count].rearrange("p f (c n) -> p c f n", n=4)
 
-            nc.scalar.copy(out=side_by_side(1), in_=row_by_row(1))
-            nc.vector.tensor_copy(out=side_by_side(0), in_=row_by_row(0))
+        def regroup_scalar(name, g, first, count):
+            nc.scalar.copy(out=side_by_side(name, g, first, count), in_=row_by_row(name, g, first, count))
 
-        def quantise(name, i):
-            width = WINDOWS[i][2]
-            slot = SLOTS[i]
-            for g in (1, 0):
-                nc.vector.quantize_mx(
-                    out=w_codes[name][:, g, slot : slot + width].bitcast(FP8X4),
-                    scales=w_scales[name][:, g, slot : slot + width],
-                    in_=w_stage[(i, g)][:].rearrange("p c f -> p (c f)"),
-                )
+        def regroup_vector(name, g, first, count):
+            nc.vector.tensor_copy(out=side_by_side(name, g, first, count), in_=row_by_row(name, g, first, count))
 
-        def prepare_weights(name):
-            for i in range(len(WINDOWS) + 1):
-                if i < len(WINDOWS):
-                    regroup(name, i)
-                if i > 0:
-                    quantise(name, i - 1)
+        def quantise(name, g, first, count):
+            nc.vector.quantize_mx(
+                out=w_codes[name][:, g, first : first + count].bitcast(FP8X4),
+                scales=w_scales[name][:, g, first : first + count],
+                in_=w_stage[(name, g)][:, first : first + count, :].rearrange("p c f -> p (c f)"),
+            )
 
         def project(name, t):
             banks = []
-            for i in range(len(WINDOWS)):
-                width = WINDOWS[i][2]
-                slot = SLOTS[i]
-                banks.append(psum.tile([P, BANK], F32, name="y", tag="bank"))
+            for first, width, first_head, heads in WINDOWS:
+                bank = psum.tile([P, BANK], F32, name="y", tag="bank")
                 for g in range(PASSES):
                     nc.tensor.matmul_mx(
-                        out=banks[i][:, 0:width],
+                        out=bank[:, 0:width],
                         lhsT=x_codes[:, t, g * P : (g + 1) * P].bitcast(FP8X4),
                         lhsT_scale=x_scales[:, t, g * P : (g + 1) * P],
-                        rhs=w_codes[name][:, g, slot : slot + width].bitcast(FP8X4),
-                        rhs_scale=w_scales[name][:, g, slot : slot + width],
+                        rhs=w_codes[name][:, g, first : first + width].bitcast(FP8X4),
+                        rhs_scale=w_scales[name][:, g, first : first + width],
                         start=(g == 0),
                         stop=(g == PASSES - 1),
                     )
+                start = first_head * HEAD_DIM - first
+                banks.append((bank[:, start : start + heads * HEAD_DIM], first_head, heads))
 
             squares = work.tile([P, HEADS, HEAD_DIM], BF16, name="squares", bufs=2)
             sumsq = work.tile([P, HEADS], F32, name="sumsq")
-            for i in range(len(WINDOWS)):
-                first_head, heads, width = WINDOWS[i]
+            for y, first_head, heads in banks:
                 for h in range(heads):
                     nc.scalar.activation(
                         out=squares[:, first_head + h, :],
-                        in_=banks[i][:, h * HEAD_DIM : (h + 1) * HEAD_DIM],
+                        in_=y[:, h * HEAD_DIM : (h + 1) * HEAD_DIM],
                         func=ACT.Square,
                         accum_out=sumsq[:, first_head + h : first_head + h + 1],
                     )
@@ -212,54 +205,69 @@ def tile_torchgemma4visionattention_pa_kernel(
                 out=rstd[:], in_=sumsq[:], func=ACT.Abs_reciprocal_sqrt, scale=1.0 / HEAD_DIM, bias=eps_sb[:]
             )
 
-            result = work.tile([P, HEADS, HEAD_DIM], F32, name="result", bufs=5)
             if name == "v":
-                for i in range(len(WINDOWS)):
-                    first_head, heads, width = WINDOWS[i]
+                result = work.tile([P, HEADS, HEAD_DIM], F32, name="result", bufs=5)
+                for y, first_head, heads in banks:
                     nc.vector.tensor_tensor(
                         out=result[:, first_head : first_head + heads, :],
-                        in0=banks[i][:, 0 : heads * HEAD_DIM].rearrange("p (h j) -> p h j", j=HEAD_DIM),
+                        in0=y.rearrange("p (h j) -> p h j", j=HEAD_DIM),
                         in1=rstd[:, first_head : first_head + heads].unsqueeze(2).to_broadcast([P, heads, HEAD_DIM]),
                         op=MULT,
                     )
-            else:
-                products = work.tile([P, HEADS, 2, HEAD_DIM], F32, name="products", bufs=2)
-                for i in range(len(WINDOWS)):
-                    first_head, heads, width = WINDOWS[i]
-                    for h in range(heads):
-                        nc.vector.scalar_tensor_tensor(
-                            out=products[:, first_head + h, :, :],
-                            in0=banks[i][:, h * HEAD_DIM : (h + 1) * HEAD_DIM].unsqueeze(1).to_broadcast([P, 2, HEAD_DIM]),
-                            scalar=rstd[:, first_head + h : first_head + h + 1],
-                            in1=rope[name][:, t, :, :],
-                            op0=MULT,
-                            op1=MULT,
-                        )
-                result5 = result[:].rearrange("p h (a b i) -> p h a b i", a=2, b=2)
-                products6 = products[:].rearrange("p h s (a b i) -> p h s a b i", a=2, b=2)
-                for b in range(2):
-                    nc.gpsimd.tensor_tensor(
-                        out=result5[:, :, :, b, :],
-                        in0=products6[:, :, 0, :, b, :],
-                        in1=products6[:, :, 1, :, 1 - b, :],
-                        op=ADD,
+                return result
+            products = work.tile([P, HEADS, 2, HEAD_DIM], F32, name="products", bufs=2)
+            for y, first_head, heads in banks:
+                for h in range(heads):
+                    nc.vector.scalar_tensor_tensor(
+                        out=products[:, first_head + h, :, :],
+                        in0=y[:, h * HEAD_DIM : (h + 1) * HEAD_DIM].unsqueeze(1).to_broadcast([P, 2, HEAD_DIM]),
+                        scalar=rstd[:, first_head + h : first_head + h + 1],
+                        in1=rope[name][:, t, :, :],
+                        op0=MULT,
+                        op1=MULT,
                     )
+            return products
+
+        def add_products(products):
+            result = work.tile([P, HEADS, HEAD_DIM], F32, name="result", bufs=5)
+            result5 = result[:].rearrange("p h (a b i) -> p h a b i", a=2, b=2)
+            products6 = products[:].rearrange("p h s (a b i) -> p h s a b i", a=2, b=2)
+            for b in range(2):
+                nc.gpsimd.tensor_tensor(
+                    out=result5[:, :, :, b, :],
+                    in0=products6[:, :, 0, :, b, :],
+                    in1=products6[:, :, 1, :, 1 - b, :],
+                    op=ADD,
+                )
             return result
 
         def store(name, t, result):
             nc.sync.dma_start(out=outputs[name].rearrange("(p t) h j -> p t h j", t=TILES)[:, t, :, :], in_=result[:])
 
+        def prepare_weights(name):
+            new_stage(name)
+            for i in range(len(PIECES) + 1):
+                if i < len(PIECES):
+                    regroup_scalar(name, 1, *PIECES[i])
+                    regroup_vector(name, 0, *PIECES[i])
+                if i > 0:
+                    for g in (1, 0):
+                        quantise(name, g, *PIECES[i - 1])
+
+        def prepare_tokens(first):
+            quantise_tokens(first, turn_tokens(first))
+
         build_rope_table("q")
+        build_rope_table("k")
         prepare_weights("q")
         prepare_tokens(0)
-        build_rope_table("k")
         prepare_weights("k")
         prepare_weights("v")
         for t in range(TILES):
-            results = {}
-            for name in ("q", "k", "v"):
-                results[name] = project(name, t)
-            for name in ("q", "v", "k"):
-                store(name, t, results[name])
+            for name in ("q", "k"):
+                store(name, t, add_products(project(name, t)))
+            if t > 0:
+                store("v", t - 1, project("v", t - 1))
             if t % PAIR == 0 and t + PAIR < TILES:
                 prepare_tokens(t + PAIR)
+        store("v", TILES - 1, project("v", TILES - 1))

@@ -30,6 +30,7 @@ BANK = 512
 
 WINDOWS = ((0, 512, 0, 7), (448, 512, 7, 6), (896, 256, 13, 3))
 PIECES = ((0, 512), (512, 512), (1024, 128))
+GAIN_PITCH = 96
 PAIR = 2
 
 FLOPS = 2 * TOKENS * D_MODEL * 3 * FEATURES
@@ -71,18 +72,20 @@ def tile_torchgemma4visionattention_pa_kernel(
 
         cos_sb = keep.tile([P, TILES, HEAD_DIM], BF16, name="cos_sb")
         sin_sb = keep.tile([P, TILES, HEAD_DIM], BF16, name="sin_sb")
-        nc.sync.dma_start(out=cos_sb[:], in_=cos.rearrange("(p t) j -> p t j", t=TILES))
-        nc.sync.dma_start(out=sin_sb[:], in_=sin.rearrange("(p t) j -> p t j", t=TILES))
-        gain_sb = {}
-        for name in ("q", "k"):
-            gain_sb[name] = keep.tile([P, HEAD_DIM], BF16, name="gain_" + name)
-            nc.sync.dma_start(out=gain_sb[name][:], in_=gains[name].partition_broadcast(P))
+        gain_rows = keep.tile([P, 2, GAIN_PITCH], BF16, name="gain_rows")
+        nc.gpsimd.memset(gain_rows[:], 0.0)
+        ones = keep.tile([P, P], BF16, name="ones")
+        nc.gpsimd.memset(ones[:], 1.0)
+        for n, name in ((0, "q"), (1, "k")):
+            nc.scalar.dma_start(out=gain_rows[0:1, n, 0:HEAD_DIM], in_=gains[name].unsqueeze(0))
 
         new_raw("q")
         for first, count in PIECES:
             for g in (1, 0):
                 load_weight("q", g, first, count)
         load_tokens(0, PAIR)
+        nc.sync.dma_start(out=cos_sb[:], in_=cos.rearrange("(p t) j -> p t j", t=TILES))
+        nc.sync.dma_start(out=sin_sb[:], in_=sin.rearrange("(p t) j -> p t j", t=TILES))
         for name in ("k", "v"):
             new_raw(name)
             for g in (1, 0):
@@ -97,10 +100,21 @@ def tile_torchgemma4visionattention_pa_kernel(
         nc.scalar.activation(out=warm[:], in_=eps_sb[:], func=ACT.Abs_reciprocal_sqrt)
 
         rope = {}
+        gain_sb = {}
+
+        def spread_gains():
+            bank = psum.tile([P, BANK], F32, name="gain_bank", tag="bank")
+            nc.tensor.matmul(
+                bank[:, 0 : 2 * GAIN_PITCH], lhsT=ones[:], rhs=gain_rows[:].rearrange("p n j -> p (n j)"), start=True, stop=True
+            )
+            both = keep.tile([P, 2, GAIN_PITCH], F32, name="gains_spread")
+            nc.scalar.copy(out=both[:].rearrange("p n j -> p (n j)"), in_=bank[:, 0 : 2 * GAIN_PITCH])
+            for n, name in ((0, "q"), (1, "k")):
+                gain_sb[name] = both[:, n, 0:HEAD_DIM]
 
         def build_rope_table(name):
             signed = keep.tile([P, 2, 2, ROT], F32, name="signed_" + name)
-            gain4 = gain_sb[name][:].rearrange("p (a b i) -> p a b i", a=2, b=2)
+            gain4 = gain_sb[name].rearrange("p (a b i) -> p a b i", a=2, b=2)
             for b, sign in ((0, 1.0), (1, -1.0)):
                 nc.vector.tensor_scalar(
                     out=signed[:, :, b, :], in0=gain4[:, :, b, :], scalar1=sign, scalar2=0.0, op0=MULT, op1=ADD
@@ -109,7 +123,7 @@ def tile_torchgemma4visionattention_pa_kernel(
             nc.vector.tensor_tensor(
                 out=rope[name][:, :, 0, :],
                 in0=cos_sb[:],
-                in1=gain_sb[name][:].unsqueeze(1).to_broadcast([P, TILES, HEAD_DIM]),
+                in1=gain_sb[name].unsqueeze(1).to_broadcast([P, TILES, HEAD_DIM]),
                 op=MULT,
             )
             cross5 = rope[name][:, :, 1, :].rearrange("p t (a b i) -> p t a b i", a=2, b=2)
@@ -257,10 +271,11 @@ def tile_torchgemma4visionattention_pa_kernel(
         def prepare_tokens(first):
             quantise_tokens(first, turn_tokens(first))
 
-        build_rope_table("q")
-        build_rope_table("k")
         prepare_weights("q")
         prepare_tokens(0)
+        spread_gains()
+        build_rope_table("q")
+        build_rope_table("k")
         prepare_weights("k")
         prepare_weights("v")
         for t in range(TILES):

@@ -218,17 +218,28 @@ def tile_torchgemma4visionattention_pa_kernel(
             nc.scalar.activation(
                 out=rstd[:], in_=sumsq[:], func=ACT.Abs_reciprocal_sqrt, scale=1.0 / HEAD_DIM, bias=eps_sb[:]
             )
+            return banks, rstd
 
-            if name == "v":
-                result = work.tile([P, HEADS, HEAD_DIM], F32, name="result", bufs=5)
-                for y, first_head, heads in banks:
-                    nc.vector.tensor_tensor(
-                        out=result[:, first_head : first_head + heads, :],
-                        in0=y.rearrange("p (h j) -> p h j", j=HEAD_DIM),
-                        in1=rstd[:, first_head : first_head + heads].unsqueeze(2).to_broadcast([P, heads, HEAD_DIM]),
-                        op=MULT,
+        def scale_on_vector(banks, rstd, result):
+            for y, first_head, heads in banks:
+                nc.vector.tensor_tensor(
+                    out=result[:, first_head : first_head + heads, :],
+                    in0=y.rearrange("p (h j) -> p h j", j=HEAD_DIM),
+                    in1=rstd[:, first_head : first_head + heads].unsqueeze(2).to_broadcast([P, heads, HEAD_DIM]),
+                    op=MULT,
+                )
+
+        def scale_on_scalar(banks, rstd, result):
+            for y, first_head, heads in banks:
+                for h in range(heads):
+                    nc.scalar.activation(
+                        out=result[:, first_head + h, :],
+                        in_=y[:, h * HEAD_DIM : (h + 1) * HEAD_DIM],
+                        func=ACT.Copy,
+                        scale=rstd[:, first_head + h : first_head + h + 1],
                     )
-                return result
+
+        def multiply_by_tables(name, t, banks, rstd):
             products = work.tile([P, HEADS, 2, HEAD_DIM], F32, name="products", bufs=2)
             for y, first_head, heads in banks:
                 for h in range(heads):
@@ -242,21 +253,36 @@ def tile_torchgemma4visionattention_pa_kernel(
                     )
             return products
 
-        def add_products(products):
-            result = work.tile([P, HEADS, HEAD_DIM], F32, name="result", bufs=5)
+        def add_products(engine, products, result, begin, end):
             result5 = result[:].rearrange("p h (a b i) -> p h a b i", a=2, b=2)
             products6 = products[:].rearrange("p h s (a b i) -> p h s a b i", a=2, b=2)
             for b in range(2):
-                nc.gpsimd.tensor_tensor(
-                    out=result5[:, :, :, b, :],
-                    in0=products6[:, :, 0, :, b, :],
-                    in1=products6[:, :, 1, :, 1 - b, :],
+                engine.tensor_tensor(
+                    out=result5[:, begin:end, :, b, :],
+                    in0=products6[:, begin:end, 0, :, b, :],
+                    in1=products6[:, begin:end, 1, :, 1 - b, :],
                     op=ADD,
                 )
-            return result
 
-        def store(name, t, result):
-            nc.sync.dma_start(out=outputs[name].rearrange("(p t) h j -> p t h j", t=TILES)[:, t, :, :], in_=result[:])
+        def store(name, t, result, begin=0, end=HEADS):
+            rows = outputs[name].rearrange("(p t) h j -> p t h j", t=TILES)
+            nc.sync.dma_start(out=rows[:, t, begin:end, :], in_=result[:, begin:end, :])
+
+        def normalise(t):
+            banks, rstd = project("v", t)
+            result = new_result()
+            scale_on_vector(banks, rstd, result)
+            store("v", t, result)
+
+        def rotate(name, t):
+            products = multiply_by_tables(name, t, *project(name, t))
+            result = new_result()
+            add_products(nc.gpsimd, products, result, 0, HEADS)
+            store(name, t, result)
+
+        def new_result():
+            result = work.tile([P, HEADS, HEAD_DIM], F32, name="result", bufs=5)
+            return result
 
         def prepare_weights(name):
             new_stage(name)
@@ -278,11 +304,25 @@ def tile_torchgemma4visionattention_pa_kernel(
         build_rope_table("k")
         prepare_weights("k")
         prepare_weights("v")
-        for t in range(TILES):
+        for t in range(TILES - 1):
             for name in ("q", "k"):
-                store(name, t, add_products(project(name, t)))
+                rotate(name, t)
             if t > 0:
-                store("v", t - 1, project("v", t - 1))
+                normalise(t - 1)
             if t % PAIR == 0 and t + PAIR < TILES:
                 prepare_tokens(t + PAIR)
-        store("v", TILES - 1, project("v", TILES - 1))
+        last = TILES - 1
+        rotate("q", last)
+        normalise(last - 1)
+        products = multiply_by_tables("k", last, *project("k", last))
+        banks, rstd = project("v", last)
+        result = new_result()
+        split = WINDOWS[0][3]
+        add_products(nc.gpsimd, products, result, 0, split)
+        store("k", last, result, 0, split)
+        add_products(nc.vector, products, result, split, HEADS)
+        store("k", last, result, split, HEADS)
+        result = new_result()
+        scale_on_vector(banks[0:1], rstd, result)
+        scale_on_scalar(banks[1:], rstd, result)
+        store("v", last, result)

@@ -169,10 +169,10 @@ def tile_torchgemma4visionattention_pa_kernel(
                 w_stage[(name, g)] = stage.tile([P, FEATURES, PACK], BF16, name="w_stage_%d" % g, align_bytes=64)
 
         def side_by_side(name, g, first, count):
-            return w_stage[(name, g)][:, first : first + count, :].rearrange("p (c n) f -> p c f n", n=4)
+            return w_stage[(name, g)][:, first : first + count, :].rearrange("p (c n) f -> p c f n", n=2)
 
         def row_by_row(name, g, first, count):
-            return w_raw[name][:, g, :, first : first + count].rearrange("p f (c n) -> p c f n", n=4)
+            return w_raw[name][:, g, :, first : first + count].rearrange("p f (c n) -> p c f n", n=2)
 
         def regroup_scalar(name, g, first, count):
             nc.scalar.copy(out=side_by_side(name, g, first, count), in_=row_by_row(name, g, first, count))

@@ -47,7 +47,7 @@ def tile_torchgemma4visionattention_pa_kernel(
     with ExitStack() as ctx:
         ctx.enter_context(tc.manual_schedule())
         keep = ctx.enter_context(tc.tile_pool(name="keep", bufs=1))
-        raws = ctx.enter_context(tc.tile_pool(name="raws", bufs=3))
+        raws = ctx.enter_context(tc.tile_pool(name="raws", bufs=2))
         stage = ctx.enter_context(tc.tile_pool(name="stage", bufs=2))
         work = ctx.enter_context(tc.tile_pool(name="work", bufs=3))
         psum = ctx.enter_context(tc.psum_pool(name="psum", bufs=8))
@@ -86,11 +86,9 @@ def tile_torchgemma4visionattention_pa_kernel(
         load_tokens(0, PAIR)
         nc.sync.dma_start(out=cos_sb[:], in_=cos.rearrange("(p t) j -> p t j", t=TILES))
         nc.sync.dma_start(out=sin_sb[:], in_=sin.rearrange("(p t) j -> p t j", t=TILES))
-        for name in ("k", "v"):
-            new_raw(name)
-            for g in (1, 0):
-                load_weight(name, g, 0, FEATURES)
-        load_tokens(PAIR, TILES - PAIR)
+        new_raw("k")
+        for g in (1, 0):
+            load_weight("k", g, 0, FEATURES)
 
         ident = keep.tile([P, P], F32, name="ident")
         make_identity(nc, ident[:])
@@ -150,6 +148,23 @@ def tile_torchgemma4visionattention_pa_kernel(
                 nc.scalar.copy(out=x_grouped[:, n].bitcast(F32), in_=turned[:].rearrange("p g u r -> p g r u"))
             return x_grouped
 
+        def turn_tile(t):
+            x_one = stage.tile([P, PASSES, P, PACK], BF16, name="x_one", align_bytes=64)
+            x_words = x_sb[:, t, :].bitcast(F32).rearrange("r (g p u) -> r g u p", g=PASSES, u=2)
+            turned = psum.tile([P, PASSES, 2, P], F32, name="turned", tag="bank")
+            for g in range(PASSES):
+                for u in range(2):
+                    nc.tensor.transpose(turned[:, g, u, :], x_words[:, g, u, :], ident[:])
+            nc.scalar.copy(out=x_one[:].bitcast(F32), in_=turned[:].rearrange("p g u r -> p g r u"))
+            return x_one
+
+        def quantise_tile(t, x_one):
+            nc.vector.quantize_mx(
+                out=x_codes[:, t, :].bitcast(FP8X4),
+                scales=x_scales[:, t, :],
+                in_=x_one[:].rearrange("p g r f -> p (g r f)"),
+            )
+
         def quantise_tokens(first, x_grouped):
             nc.vector.quantize_mx(
                 out=x_codes[:, first : first + PAIR, :].rearrange("p t c -> p (t c)").bitcast(FP8X4),
@@ -187,71 +202,91 @@ def tile_torchgemma4visionattention_pa_kernel(
                 in_=w_stage[(name, g)][:, first : first + count, :].rearrange("p c f -> p (c f)"),
             )
 
-        def project(name, t):
-            banks = []
-            for first, width, first_head, heads in WINDOWS:
-                bank = psum.tile([P, BANK], F32, name="y", tag="bank")
-                for g in range(PASSES):
-                    nc.tensor.matmul_mx(
-                        out=bank[:, 0:width],
-                        lhsT=x_codes[:, t, g * P : (g + 1) * P].bitcast(FP8X4),
-                        lhsT_scale=x_scales[:, t, g * P : (g + 1) * P],
-                        rhs=w_codes[name][:, g, first : first + width].bitcast(FP8X4),
-                        rhs_scale=w_scales[name][:, g, first : first + width],
-                        start=(g == 0),
-                        stop=(g == PASSES - 1),
-                    )
-                start = first_head * HEAD_DIM - first
-                banks.append((bank[:, start : start + heads * HEAD_DIM], first_head, heads))
+        bank_of = {}
+        sumsq_of = {}
+        rstd_of = {}
+        junk_of = {}
 
-            squares = work.tile([P, HEADS, HEAD_DIM], BF16, name="squares", bufs=2)
-            sumsq = work.tile([P, HEADS], F32, name="sumsq")
-            for y, first_head, heads in banks:
-                for h in range(heads):
-                    nc.scalar.activation(
-                        out=squares[:, first_head + h, :],
-                        in_=y[:, h * HEAD_DIM : (h + 1) * HEAD_DIM],
-                        func=ACT.Square,
-                        accum_out=sumsq[:, first_head + h : first_head + h + 1],
-                    )
-            rstd = work.tile([P, HEADS], F32, name="rstd")
-            nc.scalar.activation(
-                out=rstd[:], in_=sumsq[:], func=ACT.Abs_reciprocal_sqrt, scale=1.0 / HEAD_DIM, bias=eps_sb[:]
-            )
-            return banks, rstd
+        def heads_of(name, t, w):
+            first, width, first_head, heads = WINDOWS[w]
+            start = first_head * HEAD_DIM - first
+            return bank_of[(name, t, w)][:, start : start + heads * HEAD_DIM]
 
-        def scale_on_vector(banks, rstd, result):
-            for y, first_head, heads in banks:
-                nc.vector.tensor_tensor(
-                    out=result[:, first_head : first_head + heads, :],
-                    in0=y.rearrange("p (h j) -> p h j", j=HEAD_DIM),
-                    in1=rstd[:, first_head : first_head + heads].unsqueeze(2).to_broadcast([P, heads, HEAD_DIM]),
-                    op=MULT,
+        def multiply(name, t, w):
+            first, width, first_head, heads = WINDOWS[w]
+            bank = psum.tile([P, BANK], F32, name="y", tag="bank")
+            bank_of[(name, t, w)] = bank
+            for g in range(PASSES):
+                nc.tensor.matmul_mx(
+                    out=bank[:, 0:width],
+                    lhsT=x_codes[:, t, g * P : (g + 1) * P].bitcast(FP8X4),
+                    lhsT_scale=x_scales[:, t, g * P : (g + 1) * P],
+                    rhs=w_codes[name][:, g, first : first + width].bitcast(FP8X4),
+                    rhs_scale=w_scales[name][:, g, first : first + width],
+                    start=(g == 0),
+                    stop=(g == PASSES - 1),
                 )
 
-        def scale_on_scalar(banks, rstd, result):
-            for y, first_head, heads in banks:
-                for h in range(heads):
-                    nc.scalar.activation(
-                        out=result[:, first_head + h, :],
-                        in_=y[:, h * HEAD_DIM : (h + 1) * HEAD_DIM],
-                        func=ACT.Copy,
-                        scale=rstd[:, first_head + h : first_head + h + 1],
-                    )
+        def root(name, t, source):
+            rstd = work.tile([P, HEADS], F32, name="rstd", bufs=4)
+            rstd_of[(name, t)] = rstd
+            nc.scalar.activation(
+                out=rstd[:], in_=source, func=ACT.Abs_reciprocal_sqrt, scale=1.0 / HEAD_DIM, bias=eps_sb[:]
+            )
 
-        def multiply_by_tables(name, t, banks, rstd):
-            products = work.tile([P, HEADS, 2, HEAD_DIM], F32, name="products", bufs=2)
-            for y, first_head, heads in banks:
-                for h in range(heads):
-                    nc.vector.scalar_tensor_tensor(
-                        out=products[:, first_head + h, :, :],
-                        in0=y[:, h * HEAD_DIM : (h + 1) * HEAD_DIM].unsqueeze(1).to_broadcast([P, 2, HEAD_DIM]),
-                        scalar=rstd[:, first_head + h : first_head + h + 1],
-                        in1=rope[name][:, t, :, :],
-                        op0=MULT,
-                        op1=MULT,
-                    )
+        def square_heads(name, t, w):
+            first, width, first_head, heads = WINDOWS[w]
+            y = heads_of(name, t, w)
+            if w == 0:
+                sumsq = work.tile([P, HEADS], F32, name="sumsq", bufs=2)
+                sumsq_of[(name, t)] = sumsq
+            if w == 0:
+                junk = work.tile([P, HEADS, HEAD_DIM], BF16, name="junk", bufs=2)
+                junk_of[(name, t)] = junk
+            for h in range(heads):
+                nc.scalar.activation(
+                    out=junk_of[(name, t)][:, first_head + h, :], in_=y[:, h * HEAD_DIM : (h + 1) * HEAD_DIM], func=ACT.Square,
+                    accum_out=sumsq_of[(name, t)][:, first_head + h : first_head + h + 1],
+                )
+
+        def scale_scalar(name, t, w, result):
+            first, width, first_head, heads = WINDOWS[w]
+            y = heads_of(name, t, w)
+            for h in range(heads):
+                nc.scalar.activation(
+                    out=result[:, first_head + h, :], in_=y[:, h * HEAD_DIM : (h + 1) * HEAD_DIM], func=ACT.Copy,
+                    scale=rstd_of[(name, t)][:, first_head + h : first_head + h + 1],
+                )
+
+        def scale_vector(name, t, w, result):
+            first, width, first_head, heads = WINDOWS[w]
+            nc.vector.tensor_tensor(
+                out=result[:, first_head : first_head + heads, :],
+                in0=heads_of(name, t, w).rearrange("p (h j) -> p h j", j=HEAD_DIM),
+                in1=rstd_of[(name, t)][:, first_head : first_head + heads].unsqueeze(2).to_broadcast([P, heads, HEAD_DIM]),
+                op=MULT,
+            )
+
+        def new_result():
+            result = work.tile([P, HEADS, HEAD_DIM], F32, name="result", bufs=6)
+            return result
+
+        def new_products():
+            products = work.tile([P, HEADS, 2, HEAD_DIM], F32, name="products", bufs=3)
             return products
+
+        def turn(name, t, w, products):
+            first, width, first_head, heads = WINDOWS[w]
+            y = heads_of(name, t, w)
+            for h in range(heads):
+                nc.vector.scalar_tensor_tensor(
+                    out=products[:, first_head + h, :, :],
+                    in0=y[:, h * HEAD_DIM : (h + 1) * HEAD_DIM].unsqueeze(1).to_broadcast([P, 2, HEAD_DIM]),
+                    scalar=rstd_of[(name, t)][:, first_head + h : first_head + h + 1],
+                    in1=rope[name][:, t, :, :],
+                    op0=MULT,
+                    op1=MULT,
+                )
 
         def add_products(engine, products, result, begin, end):
             result5 = result[:].rearrange("p h (a b i) -> p h a b i", a=2, b=2)
@@ -268,61 +303,95 @@ def tile_torchgemma4visionattention_pa_kernel(
             rows = outputs[name].rearrange("(p t) h j -> p t h j", t=TILES)
             nc.sync.dma_start(out=rows[:, t, begin:end, :], in_=result[:, begin:end, :])
 
-        def normalise(t):
-            banks, rstd = project("v", t)
-            result = new_result()
-            scale_on_vector(banks, rstd, result)
-            store("v", t, result)
+        def prep(name, i, pieces=PIECES):
+            first, count = pieces[i]
+            regroup_scalar(name, 1, first, count)
+            regroup_vector(name, 0, first, count)
+
+        def prepare_weights(name, pieces=PIECES):
+            new_stage(name)
+            for i in range(len(pieces) + 1):
+                if i < len(pieces):
+                    prep(name, i, pieces)
+                if i > 0:
+                    for g in (1, 0):
+                        quantise(name, g, *pieces[i - 1])
+
+        def heads_all(name, t):
+            for w in range(3):
+                square_heads(name, t, w)
+            root(name, t, sumsq_of[(name, t)][:])
 
         def rotate(name, t):
-            products = multiply_by_tables(name, t, *project(name, t))
+            products = new_products()
+            for w in range(3):
+                turn(name, t, w, products)
             result = new_result()
             add_products(nc.gpsimd, products, result, 0, HEADS)
             store(name, t, result)
 
-        def new_result():
-            result = work.tile([P, HEADS, HEAD_DIM], F32, name="result", bufs=5)
-            return result
+        def scale(t):
+            result = new_result()
+            for w in range(3):
+                scale_vector("v", t, w, result)
+            store("v", t, result)
 
-        def prepare_weights(name):
-            new_stage(name)
-            for i in range(len(PIECES) + 1):
-                if i < len(PIECES):
-                    regroup_scalar(name, 1, *PIECES[i])
-                    regroup_vector(name, 0, *PIECES[i])
-                if i > 0:
-                    for g in (1, 0):
-                        quantise(name, g, *PIECES[i - 1])
+        def mx(name, t):
+            for w in range(3):
+                multiply(name, t, w)
 
-        def prepare_tokens(first):
-            quantise_tokens(first, turn_tokens(first))
-
-        prepare_weights("q")
-        prepare_tokens(0)
+        prepare_weights("q", PIECES)
+        new_raw("v")
+        for g in (1, 0):
+            load_weight("v", g, 0, FEATURES)
+        load_tokens(PAIR, TILES - PAIR)
+        quantise_tokens(0, turn_tokens(0))
         spread_gains()
         build_rope_table("q")
         build_rope_table("k")
         prepare_weights("k")
         prepare_weights("v")
+        mx("q", 0)
+        heads_all("q", 0)
         for t in range(TILES - 1):
-            for name in ("q", "k"):
-                rotate(name, t)
             if t > 0:
-                normalise(t - 1)
-            if t % PAIR == 0 and t + PAIR < TILES:
-                prepare_tokens(t + PAIR)
+                mx("q", t)
+                heads_all("q", t)
+            rotate("q", t)
+            if t + 2 < TILES:
+                one = turn_tile(t + 2)
+            mx("k", t)
+            heads_all("k", t)
+            rotate("k", t)
+            if t + 2 < TILES:
+                quantise_tile(t + 2, one)
+            if t > 0:
+                mx("v", t - 1)
+                heads_all("v", t - 1)
+                scale(t - 1)
         last = TILES - 1
+        mx("q", last)
+        heads_all("q", last)
         rotate("q", last)
-        normalise(last - 1)
-        products = multiply_by_tables("k", last, *project("k", last))
-        banks, rstd = project("v", last)
-        result = new_result()
+        mx("k", last)
+        heads_all("k", last)
+        products = new_products()
+        k_result = new_result()
+        for w in range(3):
+            turn("k", last, w, products)
         split = WINDOWS[0][3]
-        add_products(nc.gpsimd, products, result, 0, split)
-        store("k", last, result, 0, split)
-        add_products(nc.vector, products, result, split, HEADS)
-        store("k", last, result, split, HEADS)
+        add_products(nc.gpsimd, products, k_result, 0, split)
+        mx("v", last - 1)
+        heads_all("v", last - 1)
+        scale(last - 1)
+        store("k", last, k_result, 0, split)
+        add_products(nc.vector, products, k_result, split, HEADS)
+        store("k", last, k_result, split, HEADS)
+        mx("v", last)
+        heads_all("v", last)
         result = new_result()
-        scale_on_vector(banks[0:1], rstd, result)
-        scale_on_scalar(banks[1:], rstd, result)
-        store("v", last, result)
+        scale_scalar("v", last, 1, result)
+        scale_scalar("v", last, 2, result)
+        store("v", last, result, split, HEADS)
+        scale_vector("v", last, 0, result)
+        store("v", last, result, 0, split)

@@ -92,6 +92,8 @@ def tile_torchgemma4visionattention_pa_kernel(
 
         ident = keep.tile([P, P], F32, name="ident")
         make_identity(nc, ident[:])
+        ident_bf = keep.tile([P, P], BF16, name="ident_bf")
+        nc.gpsimd.tensor_copy(out=ident_bf[:], in_=ident[:])
         eps_sb = keep.tile([P, 1], F32, name="eps_sb")
         nc.vector.memset(eps_sb[:], EPS)
         warm = keep.tile([P, 1], F32, name="warm")
@@ -191,6 +193,23 @@ def tile_torchgemma4visionattention_pa_kernel(
 
         def regroup_scalar(name, g, first, count):
             nc.scalar.copy(out=side_by_side(name, g, first, count), in_=row_by_row(name, g, first, count))
+
+        def regroup_tensor(name, g, first, count):
+            bank = psum.tile([P, BANK], F32, name="regrouped", tag="bank")
+            view = bank[:, 0 : 2 * count].bitcast(BF16).rearrange("p (c f) -> p f c", f=PACK)
+            rows = min(PACK, BANK // count)
+            for f in range(0, PACK, rows):
+                nc.tensor.matmul(
+                    out=view[:, f : f + rows, :],
+                    lhsT=ident_bf[:],
+                    rhs=w_raw[name][:, g, f : f + rows, first : first + count],
+                    start=True,
+                    stop=True,
+                )
+            nc.scalar.copy(
+                out=w_stage[(name, g)][:, first : first + count, :].rearrange("p c f -> p (c f)").bitcast(F32),
+                in_=bank[:, 0 : 2 * count],
+            )
 
         def regroup_vector(name, g, first, count):
             nc.vector.tensor_copy(out=side_by_side(name, g, first, count), in_=row_by_row(name, g, first, count))
@@ -305,8 +324,11 @@ def tile_torchgemma4visionattention_pa_kernel(
 
         def prep(name, i, pieces=PIECES):
             first, count = pieces[i]
-            regroup_scalar(name, 1, first, count)
-            regroup_vector(name, 0, first, count)
+            for b in range(0, count, 256):
+                regroup_tensor(name, 1, first + b, min(256, count - b))
+            mine = int(count * 0.2) // 16 * 16
+            regroup_vector(name, 0, first, count - mine)
+            regroup_scalar(name, 0, first + count - mine, mine)
 
         def prepare_weights(name, pieces=PIECES):
             new_stage(name)
@@ -344,24 +366,33 @@ def tile_torchgemma4visionattention_pa_kernel(
         new_raw("v")
         for g in (1, 0):
             load_weight("v", g, 0, FEATURES)
-        load_tokens(PAIR, TILES - PAIR)
+        load_tokens(PAIR, PAIR)
+        load_tokens(2 * PAIR, TILES - 2 * PAIR)
         quantise_tokens(0, turn_tokens(0))
         spread_gains()
         build_rope_table("q")
         build_rope_table("k")
         prepare_weights("k")
-        prepare_weights("v")
+        new_stage("v")
+        prep("v", 0)
+        prep("v", 1)
+        for g in (1, 0):
+            quantise("v", g, *PIECES[0])
         mx("q", 0)
         heads_all("q", 0)
+        prep("v", 2)
+        for i in (1, 2):
+            for g in (1, 0):
+                quantise("v", g, *PIECES[i])
         for t in range(TILES - 1):
             if t > 0:
                 mx("q", t)
                 heads_all("q", t)
             rotate("q", t)
-            if t + 2 < TILES:
-                one = turn_tile(t + 2)
             mx("k", t)
             heads_all("k", t)
+            if t + 2 < TILES:
+                one = turn_tile(t + 2)
             rotate("k", t)
             if t + 2 < TILES:
                 quantise_tile(t + 2, one)

from contextlib import ExitStack

import concourse.mybir as mybir
from concourse.masks import make_identity

F32 = mybir.dt.float32
BF16 = mybir.dt.bfloat16
I32 = mybir.dt.int32
U32 = mybir.dt.uint32
U8 = mybir.dt.uint8
FP8X4 = mybir.dt.float8_e4m3fn_x4
MULT = mybir.AluOpType.mult
ADD = mybir.AluOpType.add
ACT = mybir.ActivationFunctionType

P = 128
TOKENS = 1024
D_MODEL = 1024
HEADS = 16
HEAD_DIM = 72
FEATURES = HEADS * HEAD_DIM
ROT = HEAD_DIM // 4
EPS = 1e-6

TILES = TOKENS // P
PACK = 4
K_PASS = P * PACK
PASSES = D_MODEL // K_PASS
BANK = 512

WINDOWS = ((0, 512, 0, 7), (448, 512, 7, 6), (896, 256, 13, 3))
PIECES = ((0, 512), (512, 512), (1024, 128))
GAIN_PITCH = 96
PAIR = 2

FLOPS = 2 * TOKENS * D_MODEL * 3 * FEATURES


def tile_torchgemma4visionattention_pa_kernel(
    tc, hidden_states, cos, sin, Wq, Wk, Wv, q_scale, k_scale, out_0, out_1, out_2
):
    nc = tc.nc
    weights = {"q": Wq, "k": Wk, "v": Wv}
    gains = {"q": q_scale, "k": k_scale}
    outputs = {"q": out_0, "k": out_1, "v": out_2}

    with ExitStack() as ctx:
        ctx.enter_context(tc.manual_schedule())
        keep = ctx.enter_context(tc.tile_pool(name="keep", bufs=1))
        raws = ctx.enter_context(tc.tile_pool(name="raws", bufs=2))
        stage = ctx.enter_context(tc.tile_pool(name="stage", bufs=2))
        work = ctx.enter_context(tc.tile_pool(name="work", bufs=3))
        psum = ctx.enter_context(tc.psum_pool(name="psum", bufs=8))

        x_sb = keep.tile([P, TILES, D_MODEL], BF16, name="x_sb")
        x_rows = hidden_states.rearrange("(p t) k -> p t k", t=TILES)

        def load_tokens(first, count):
            nc.sync.dma_start(out=x_sb[:, first : first + count, :], in_=x_rows[:, first : first + count, :])

        w_raw = {}

        def new_raw(name):
            w_raw[name] = raws.tile([P, PASSES, PACK, FEATURES], BF16, name="w_raw")

        def load_weight(name, g, first, count):
            rows = weights[name][g * K_PASS : (g + 1) * K_PASS, first : first + count]
            nc.sync.dma_start(
                out=w_raw[name][:, g, :, first : first + count],
                in_=rows.rearrange("(p f) c -> p f c", f=PACK),
            )

        cos_sb = keep.tile([P, TILES, HEAD_DIM], BF16, name="cos_sb")
        sin_sb = keep.tile([P, TILES, HEAD_DIM], BF16, name="sin_sb")
        gain_rows = keep.tile([P, 2, GAIN_PITCH], BF16, name="gain_rows")
        nc.gpsimd.memset(gain_rows[:], 0.0)
        ones = keep.tile([P, P], BF16, name="ones")
        nc.gpsimd.memset(ones[:], 1.0)
        for n, name in ((0, "q"), (1, "k")):
            nc.scalar.dma_start(out=gain_rows[0:1, n, 0:HEAD_DIM], in_=gains[name].unsqueeze(0))

        new_raw("q")
        for first, count in PIECES:
            for g in (1, 0):
                load_weight("q", g, first, count)
        load_tokens(0, PAIR)
        nc.sync.dma_start(out=cos_sb[:], in_=cos.rearrange("(p t) j -> p t j", t=TILES))
        nc.sync.dma_start(out=sin_sb[:], in_=sin.rearrange("(p t) j -> p t j", t=TILES))
        new_raw("k")
        for g in (1, 0):
            load_weight("k", g, 0, FEATURES)

        ident = keep.tile([P, P], F32, name="ident")
        make_identity(nc, ident[:])
        ident_bf = keep.tile([P, P], BF16, name="ident_bf")
        nc.gpsimd.tensor_copy(out=ident_bf[:], in_=ident[:])
        eps_sb = keep.tile([P, 1], F32, name="eps_sb")
        nc.vector.memset(eps_sb[:], EPS)
        warm = keep.tile([P, 1], F32, name="warm")
        nc.scalar.activation(out=warm[:], in_=eps_sb[:], func=ACT.Abs_reciprocal_sqrt)

        rope = {}
        gain_sb = {}

        def spread_gains():
            bank = psum.tile([P, BANK], F32, name="gain_bank", tag="bank")
            nc.tensor.matmul(
                bank[:, 0 : 2 * GAIN_PITCH], lhsT=ones[:], rhs=gain_rows[:].rearrange("p n j -> p (n j)"), start=True, stop=True
            )
            both = keep.tile([P, 2, GAIN_PITCH], F32, name="gains_spread")
            nc.scalar.copy(out=both[:].rearrange("p n j -> p (n j)"), in_=bank[:, 0 : 2 * GAIN_PITCH])
            for n, name in ((0, "q"), (1, "k")):
                gain_sb[name] = both[:, n, 0:HEAD_DIM]

        def build_rope_table(name):
            signed = keep.tile([P, 2, 2, ROT], F32, name="signed_" + name)
            gain4 = gain_sb[name].rearrange("p (a b i) -> p a b i", a=2, b=2)
            for b, sign in ((0, 1.0), (1, -1.0)):
                nc.vector.tensor_scalar(
                    out=signed[:, :, b, :], in0=gain4[:, :, b, :], scalar1=sign, scalar2=0.0, op0=MULT, op1=ADD
                )
            rope[name] = keep.tile([P, TILES, 2, HEAD_DIM], F32, name="rope_" + name)
            nc.vector.tensor_tensor(
                out=rope[name][:, :, 0, :],
                in0=cos_sb[:],
                in1=gain_sb[name].unsqueeze(1).to_broadcast([P, TILES, HEAD_DIM]),
                op=MULT,
            )
            cross5 = rope[name][:, :, 1, :].rearrange("p t (a b i) -> p t a b i", a=2, b=2)
            sin5 = sin_sb[:].rearrange("p t (a b i) -> p t a b i", a=2, b=2)
            for b in range(2):
                nc.vector.tensor_tensor(
                    out=cross5[:, :, :, b, :],
                    in0=sin5[:, :, :, 1 - b, :],
                    in1=signed[:, :, b, :].unsqueeze(1).to_broadcast([P, TILES, 2, ROT]),
                    op=MULT,
                )

        x_codes = keep.tile([P, TILES, PASSES * P], U32, name="x_codes", align_bytes=64)
        x_scales = keep.tile([P, TILES, PASSES * P], U8, name="x_scales", align_bytes=64)

        def turn_tokens(first):
            x_grouped = stage.tile([P, PAIR, PASSES, P, PACK], BF16, name="x_grouped", align_bytes=64)
            for n in range(PAIR):
                x_words = x_sb[:, first + n, :].bitcast(F32).rearrange("r (g p u) -> r g u p", g=PASSES, u=2)
                turned = psum.tile([P, PASSES, 2, P], F32, name="turned", tag="bank")
                for g in range(PASSES):
                    for u in range(2):
                        nc.tensor.transpose(turned[:, g, u, :], x_words[:, g, u, :], ident[:])
                nc.scalar.copy(out=x_grouped[:, n].bitcast(F32), in_=turned[:].rearrange("p g u r -> p g r u"))
            return x_grouped

        def turn_tile(t):
            x_one = stage.tile([P, PASSES, P, PACK], BF16, name="x_one", align_bytes=64)
            x_words = x_sb[:, t, :].bitcast(F32).rearrange("r (g p u) -> r g u p", g=PASSES, u=2)
            turned = psum.tile([P, PASSES, 2, P], F32, name="turned", tag="bank")
            for g in range(PASSES):
                for u in range(2):
                    nc.tensor.transpose(turned[:, g, u, :], x_words[:, g, u, :], ident[:])
            nc.scalar.copy(out=x_one[:].bitcast(F32), in_=turned[:].rearrange("p g u r -> p g r u"))
            return x_one

        def quantise_tile(t, x_one):
            nc.vector.quantize_mx(
                out=x_codes[:, t, :].bitcast(FP8X4),
                scales=x_scales[:, t, :],
                in_=x_one[:].rearrange("p g r f -> p (g r f)"),
            )

        def quantise_tokens(first, x_grouped):
            nc.vector.quantize_mx(
                out=x_codes[:, first : first + PAIR, :].rearrange("p t c -> p (t c)").bitcast(FP8X4),
                scales=x_scales[:, first : first + PAIR, :].rearrange("p t c -> p (t c)"),
                in_=x_grouped[:].rearrange("p t g r f -> p (t g r f)"),
            )

        w_codes = {}
        w_scales = {}
        w_stage = {}
        for name in ("q", "v", "k"):
            w_codes[name] = keep.tile([P, PASSES, FEATURES], U32, name="w_codes_" + name, align_bytes=64)
            w_scales[name] = keep.tile([P, PASSES, FEATURES], U8, name="w_scales_" + name, align_bytes=64)

        def new_stage(name):
            for g in range(PASSES):
                w_stage[(name, g)] = stage.tile([P, FEATURES, PACK], BF16, name="w_stage_%d" % g, align_bytes=64)

        def side_by_side(name, g, first, count):
            return w_stage[(name, g)][:, first : first + count, :].rearrange("p (c n) f -> p c f n", n=2)

        def row_by_row(name, g, first, count):
            return w_raw[name][:, g, :, first : first + count].rearrange("p f (c n) -> p c f n", n=2)

        def regroup_scalar(name, g, first, count):
            nc.scalar.copy(out=side_by_side(name, g, first, count), in_=row_by_row(name, g, first, count))

        def regroup_tensor(name, g, first, count):
            bank = psum.tile([P, BANK], F32, name="regrouped", tag="bank")
            view = bank[:, 0 : 2 * count].bitcast(BF16).rearrange("p (c f) -> p f c", f=PACK)
            rows = min(PACK, BANK // count)
            for f in range(0, PACK, rows):
                nc.tensor.matmul(
                    out=view[:, f : f + rows, :],
                    lhsT=ident_bf[:],
                    rhs=w_raw[name][:, g, f : f + rows, first : first + count],
                    start=True,
                    stop=True,
                )
            nc.scalar.copy(
                out=w_stage[(name, g)][:, first : first + count, :].rearrange("p c f -> p (c f)").bitcast(F32),
                in_=bank[:, 0 : 2 * count],
            )

        def regroup_vector(name, g, first, count):
            nc.vector.tensor_copy(out=side_by_side(name, g, first, count), in_=row_by_row(name, g, first, count))

        def quantise(name, g, first, count):
            nc.vector.quantize_mx(
                out=w_codes[name][:, g, first : first + count].bitcast(FP8X4),
                scales=w_scales[name][:, g, first : first + count],
                in_=w_stage[(name, g)][:, first : first + count, :].rearrange("p c f -> p (c f)"),
            )

        bank_of = {}
        sumsq_of = {}
        rstd_of = {}
        junk_of = {}

        def heads_of(name, t, w):
            first, width, first_head, heads = WINDOWS[w]
            start = first_head * HEAD_DIM - first
            return bank_of[(name, t, w)][:, start : start + heads * HEAD_DIM]

        def multiply(name, t, w):
            first, width, first_head, heads = WINDOWS[w]
            bank = psum.tile([P, BANK], F32, name="y", tag="bank")
            bank_of[(name, t, w)] = bank
            for g in range(PASSES):
                nc.tensor.matmul_mx(
                    out=bank[:, 0:width],
                    lhsT=x_codes[:, t, g * P : (g + 1) * P].bitcast(FP8X4),
                    lhsT_scale=x_scales[:, t, g * P : (g + 1) * P],
                    rhs=w_codes[name][:, g, first : first + width].bitcast(FP8X4),
                    rhs_scale=w_scales[name][:, g, first : first + width],
                    start=(g == 0),
                    stop=(g == PASSES - 1),
                )

        def root(name, t, source):
            rstd = work.tile([P, HEADS], F32, name="rstd", bufs=4)
            rstd_of[(name, t)] = rstd
            nc.scalar.activation(
                out=rstd[:], in_=source, func=ACT.Abs_reciprocal_sqrt, scale=1.0 / HEAD_DIM, bias=eps_sb[:]
            )

        def square_heads(name, t, w):
            first, width, first_head, heads = WINDOWS[w]
            y = heads_of(name, t, w)
            if w == 0:
                sumsq = work.tile([P, HEADS], F32, name="sumsq", bufs=2)
                sumsq_of[(name, t)] = sumsq
            if w == 0:
                junk = work.tile([P, HEADS, HEAD_DIM], BF16, name="junk", bufs=2)
                junk_of[(name, t)] = junk
            for h in range(heads):
                nc.scalar.activation(
                    out=junk_of[(name, t)][:, first_head + h, :], in_=y[:, h * HEAD_DIM : (h + 1) * HEAD_DIM], func=ACT.Square,
                    accum_out=sumsq_of[(name, t)][:, first_head + h : first_head + h + 1],
                )

        def scale_scalar(name, t, w, result):
            first, width, first_head, heads = WINDOWS[w]
            y = heads_of(name, t, w)
            for h in range(heads):
                nc.scalar.activation(
                    out=result[:, first_head + h, :], in_=y[:, h * HEAD_DIM : (h + 1) * HEAD_DIM], func=ACT.Copy,
                    scale=rstd_of[(name, t)][:, first_head + h : first_head + h + 1],
                )

        def scale_vector(name, t, w, result):
            first, width, first_head, heads = WINDOWS[w]
            nc.vector.tensor_tensor(
                out=result[:, first_head : first_head + heads, :],
                in0=heads_of(name, t, w).rearrange("p (h j) -> p h j", j=HEAD_DIM),
                in1=rstd_of[(name, t)][:, first_head : first_head + heads].unsqueeze(2).to_broadcast([P, heads, HEAD_DIM]),
                op=MULT,
            )

        def new_result():
            result = work.tile([P, HEADS, HEAD_DIM], F32, name="result", bufs=6)
            return result

        def new_products():
            products = work.tile([P, HEADS, 2, HEAD_DIM], F32, name="products", bufs=3)
            return products

        def turn(name, t, w, products):
            first, width, first_head, heads = WINDOWS[w]
            y = heads_of(name, t, w)
            for h in range(heads):
                nc.vector.scalar_tensor_tensor(
                    out=products[:, first_head + h, :, :],
                    in0=y[:, h * HEAD_DIM : (h + 1) * HEAD_DIM].unsqueeze(1).to_broadcast([P, 2, HEAD_DIM]),
                    scalar=rstd_of[(name, t)][:, first_head + h : first_head + h + 1],
                    in1=rope[name][:, t, :, :],
                    op0=MULT,
                    op1=MULT,
                )

        def add_products(engine, products, result, begin, end):
            result5 = result[:].rearrange("p h (a b i) -> p h a b i", a=2, b=2)
            products6 = products[:].rearrange("p h s (a b i) -> p h s a b i", a=2, b=2)
            for b in range(2):
                engine.tensor_tensor(
                    out=result5[:, begin:end, :, b, :],
                    in0=products6[:, begin:end, 0, :, b, :],
                    in1=products6[:, begin:end, 1, :, 1 - b, :],
                    op=ADD,
                )

        def store(name, t, result, begin=0, end=HEADS):
            rows = outputs[name].rearrange("(p t) h j -> p t h j", t=TILES)
            nc.sync.dma_start(out=rows[:, t, begin:end, :], in_=result[:, begin:end, :])

        def prep(name, i, pieces=PIECES):
            first, count = pieces[i]
            for b in range(0, count, 256):
                regroup_tensor(name, 1, first + b, min(256, count - b))
            mine = int(count * 0.2) // 16 * 16
            regroup_vector(name, 0, first, count - mine)
            regroup_scalar(name, 0, first + count - mine, mine)

        def prepare_weights(name, pieces=PIECES):
            new_stage(name)
            for i in range(len(pieces) + 1):
                if i < len(pieces):
                    prep(name, i, pieces)
                if i > 0:
                    for g in (1, 0):
                        quantise(name, g, *pieces[i - 1])

        def heads_all(name, t):
            for w in range(3):
                square_heads(name, t, w)
            root(name, t, sumsq_of[(name, t)][:])

        def rotate(name, t):
            products = new_products()
            for w in range(3):
                turn(name, t, w, products)
            result = new_result()
            add_products(nc.gpsimd, products, result, 0, HEADS)
            store(name, t, result)

        def scale(t):
            result = new_result()
            for w in range(3):
                scale_vector("v", t, w, result)
            store("v", t, result)

        def mx(name, t):
            for w in range(3):
                multiply(name, t, w)

        prepare_weights("q", PIECES)
        new_raw("v")
        for g in (1, 0):
            load_weight("v", g, 0, FEATURES)
        load_tokens(PAIR, PAIR)
        load_tokens(2 * PAIR, TILES - 2 * PAIR)
        quantise_tokens(0, turn_tokens(0))
        spread_gains()
        build_rope_table("q")
        build_rope_table("k")
        prepare_weights("k")
        new_stage("v")
        prep("v", 0)
        prep("v", 1)
        for g in (1, 0):
            quantise("v", g, *PIECES[0])
        mx("q", 0)
        heads_all("q", 0)
        prep("v", 2)
        for i in (1, 2):
            for g in (1, 0):
                quantise("v", g, *PIECES[i])
        for t in range(TILES - 1):
            if t > 0:
                mx("q", t)
                heads_all("q", t)
            rotate("q", t)
            mx("k", t)
            heads_all("k", t)
            if t + 2 < TILES:
                one = turn_tile(t + 2)
            rotate("k", t)
            if t + 2 < TILES:
                quantise_tile(t + 2, one)
            if t > 0:
                mx("v", t - 1)
                heads_all("v", t - 1)
                scale(t - 1)
        last = TILES - 1
        mx("q", last)
        heads_all("q", last)
        rotate("q", last)
        mx("k", last)
        heads_all("k", last)
        products = new_products()
        k_result = new_result()
        for w in range(3):
            turn("k", last, w, products)
        split = WINDOWS[0][3]
        add_products(nc.gpsimd, products, k_result, 0, split)
        mx("v", last - 1)
        heads_all("v", last - 1)
        scale(last - 1)
        store("k", last, k_result, 0, split)
        add_products(nc.vector, products, k_result, split, HEADS)
        store("k", last, k_result, split, HEADS)
        mx("v", last)
        heads_all("v", last)
        result = new_result()
        scale_scalar("v", last, 1, result)
        scale_scalar("v", last, 2, result)
        store("v", last, result, split, HEADS)
        scale_vector("v", last, 0, result)
        store("v", last, result, 0, split)
